import numpy as np
import ml_dtypes


def mxq(x, axis, fmt="e4m3"):
    dtype, down = {"e4m3": (ml_dtypes.float8_e4m3fn, 7), "e5m2": (ml_dtypes.float8_e5m2, 14)}[fmt]
    v = np.moveaxis(np.asarray(x, np.float32).astype(ml_dtypes.bfloat16).astype(np.float64), axis, -1)
    blocks = v.reshape(v.shape[:-1] + (-1, 32))
    amax = np.abs(blocks).max(-1, keepdims=True)
    byte = np.maximum(np.where(amax > 0, np.frexp(amax)[1] - 1 + 127, 0) - down, 1)
    scale = np.exp2(byte - 127.0)
    codes = (blocks / scale).astype(np.float32).astype(dtype).astype(np.float64)
    return np.moveaxis((codes * scale).reshape(v.shape), -1, axis)


WIDE = False


def mx_kscale(k):
    if not WIDE:
        return np.ones(k)
    levels = np.array([10, -10, 5, -5, 0])
    a = np.random.permutation(np.resize(levels, k // 512 * 4)).reshape(k // 512, 4)
    idx = np.arange(k)
    return np.exp2(a[idx // 512, idx % 128 // 32])


BF16 = ml_dtypes.bfloat16


def bf(x):
    return np.asarray(x, np.float32).astype(BF16)


def f64(x):
    return np.asarray(x).astype(np.float64)


B, C_IN, H, W, HID, K, C_OUT = 8, 512, 32, 32, 128, 8, 256


def setup_inputs():
    s = mx_kscale(C_IN)
    return {
        "x": bf(np.random.standard_normal((B, C_IN, H, W)) * s[None, :, None, None]),
        "w_in": bf(np.random.standard_normal((HID, C_IN)) / np.sqrt(C_IN) / s[None, :]),
        "b_in": bf(np.random.standard_normal(HID) * 0.3),
        "centers": bf(np.linspace(-2.0, 2.0, K).reshape(1, 1, K, 1, 1) + 0.1 * np.random.standard_normal((1, HID, K, 1, 1))),
        "log_widths": bf(np.random.standard_normal((1, HID, K, 1, 1)) * 0.3),
        "out_weight": bf(np.random.standard_normal((C_OUT, HID, K)) * 2.0 / np.sqrt(HID * K)),
        "out_bias": bf(np.random.standard_normal(C_OUT) * 0.3),
    }


def reference(x, w_in, b_in, centers, log_widths, out_weight, out_bias):
    xq = mxq(f64(x), 1, "e4m3")
    z = (mxq(f64(w_in), 1, "e4m3") @ xq.reshape(B, C_IN, H * W)).reshape(B, HID, H, W) + f64(b_in)[None, :, None, None]
    z = z[:, :, None, :, :]
    widths = np.logaddexp(f64(log_widths), 0.0) + 1e-4
    phi = np.exp(-(((z - f64(centers)) / widths) ** 2))
    pq = mxq(phi.reshape(B, HID * K, H * W), 1, "e4m3")
    out = (mxq(f64(out_weight).reshape(C_OUT, HID * K), 1, "e4m3") @ pq).reshape(B, C_OUT, H, W)
    return out + f64(out_bias)[None, :, None, None]

@@ -1,0 +1,292 @@
+import math
+from contextlib import ExitStack
+
+import concourse.masks as masks
+import concourse.mybir as mybir
+
+F32 = mybir.dt.float32
+BF16 = mybir.dt.bfloat16
+U32 = mybir.dt.uint32
+U8 = mybir.dt.uint8
+FP8X4 = mybir.dt.float8_e4m3fn_x4
+ACT = mybir.ActivationFunctionType
+ALU = mybir.AluOpType
+
+B, C_IN, HW, HID, K, C_OUT = 8, 512, 1024, 128, 8, 256
+P = 128
+PX = 512
+NT = B * HW // PX
+FLOPS = 2 * B * HW * (C_IN * HID + HID * K * C_OUT)
+
+
+def dve_planes(j):
+    if j == 0:
+        return (6, 7)
+    if j == NT - 1:
+        return (2, 3, 5, 6, 7)
+    return (3, 6, 7)
+
+
+def tile_rbfkanhead_t_kernel(tc, x, w_in, b_in, centers, log_widths, out_weight, out_bias, out):
+    nc = tc.nc
+    with ExitStack() as ctx:
+        const = ctx.enter_context(tc.tile_pool(name="const", bufs=1))
+        xin = ctx.enter_context(tc.tile_pool(name="xin", bufs=1))
+        work = ctx.enter_context(tc.tile_pool(name="work", bufs=3))
+        psum = ctx.enter_context(tc.psum_pool(name="psum", bufs=2))
+        ctx.enter_context(tc.manual_schedule())
+
+        lwb = const.tile([P, K], BF16)
+        cenb = const.tile([P, K], BF16)
+        binb = const.tile([P, 1], BF16)
+        ob0 = const.tile([P, 1], BF16)
+        ob1 = const.tile([P, 1], BF16)
+        with nc.allow_non_contiguous_dma(reason="small per-channel tables"):
+            nc.scalar.dma_start(out=lwb[:], in_=log_widths.rearrange("a c k x y -> (a c) (k x y)"))
+            nc.scalar.dma_start(out=cenb[:], in_=centers.rearrange("a c k x y -> (a c) (k x y)"))
+            nc.scalar.dma_start(out=binb[:], in_=b_in.rearrange("(c o) -> c o", o=1))
+            nc.scalar.dma_start(out=ob0[:], in_=out_bias[0:P].rearrange("(c o) -> c o", o=1))
+            nc.scalar.dma_start(out=ob1[:], in_=out_bias[P : 2 * P].rearrange("(c o) -> c o", o=1))
+        w_sb = const.tile([P, C_IN], BF16)
+        nc.sync.dma_start(out=w_sb[:], in_=w_in)
+        xr = []
+        for b in range(B):
+            xr.append(xin.tile([P, 4, HW], BF16, name="xr%d" % b))
+        xv = [x[b].rearrange("(p j) h w -> p j (h w)", j=4) for b in range(B)]
+        nc.sync.dma_start(out=xr[0][:, :, 0:PX], in_=xv[0][:, :, 0:PX])
+        nc.sync.dma_start(out=xr[0][:, :, PX:HW], in_=xv[0][:, :, PX:HW])
+        ow_sb = []
+        owv = out_weight.rearrange("o c k -> o (c k)")
+        for h in range(2):
+            t_ow = const.tile([P, HID * K], BF16, name="ow_sb%d" % h)
+            nc.sync.dma_start(out=t_ow[:], in_=owv[h * P : (h + 1) * P, :])
+            ow_sb.append(t_ow)
+        for b in range(1, B):
+            nc.sync.dma_start(out=xr[b][:], in_=xv[b])
+        ident = const.tile([P, P], F32)
+        masks.make_identity(nc, ident[:])
+
+        def small(nm, cols=K):
+            return const.tile([P, cols], F32, name=nm)
+
+        shift = small("shift")
+        inv = small("inv")
+        nbias = small("nbias")
+        obf = [small("obf0", 1), small("obf1", 1)]
+        wq = const.tile([P, HID], U32, align_bytes=64)
+        ws = const.tile([P, HID], U8, align_bytes=64)
+        oq = []
+        osc = []
+        xgs = {}
+        xqs = {}
+        zs = {}
+        sqs = {}
+        phis = {}
+        pqs = {}
+        ops = {}
+
+        def regroup(j, engine, q0=0, q1=4):
+            b, w0 = j // 2, (j % 2) * PX
+            if j not in xgs:
+                xgs[j] = work.tile([P, 4 * PX], BF16, tag="xg", name="xg", align_bytes=64)
+            dst = xgs[j][:, 512 * q0 : 512 * q1].rearrange("p (c i t) -> p c t i", i=4, t=4)
+            src = xr[b][:, :, w0 + 128 * q0 : w0 + 128 * q1].rearrange("p t (c i) -> p c t i", i=4)
+            if engine == "act":
+                nc.scalar.copy(out=dst, in_=src)
+            else:
+                nc.vector.tensor_copy(out=dst, in_=src)
+
+        def quant_x(j):
+            xq = work.tile([P, PX], U32, tag="xq", align_bytes=64)
+            xs = work.tile([P, PX], U8, tag="xs", align_bytes=64)
+            nc.vector.quantize_mx(out=xq[:].bitcast(FP8X4), scales=xs[:], in_=xgs[j][:])
+            xqs[j] = (xq, xs)
+
+        def mm_z(j):
+            xq, xs = xqs[j]
+            pair = []
+            for nm in ("zA", "zD"):
+                z_ps = psum.tile([P, PX], F32, tag=nm, bufs=2, name=nm)
+                nc.tensor.matmul_mx(
+                    out=z_ps[:], lhsT=wq[:].bitcast(FP8X4), lhsT_scale=ws[:],
+                    rhs=xq[:].bitcast(FP8X4), rhs_scale=xs[:], start=True, stop=True,
+                )
+                pair.append(z_ps)
+            zs[j] = pair
+
+        def sq_tile(j, g):
+            if (j, g) not in sqs:
+                sqs[(j, g)] = work.tile([P, 4, PX], F32, tag="sq", bufs=4, name="sq")
+            return sqs[(j, g)]
+
+        def square_dve(j, k):
+            uu = work.tile([P, PX], F32, tag="uu")
+            nc.vector.tensor_scalar(
+                out=uu[:], in0=zs[j][1][:], scalar1=shift[:, k : k + 1], scalar2=inv[:, k : k + 1],
+                op0=ALU.subtract, op1=ALU.mult,
+            )
+            nc.vector.tensor_tensor(out=sq_tile(j, k // 4)[:, k % 4, :], in0=uu[:], in1=uu[:], op=ALU.mult)
+
+        def squares_act(j, g):
+            for k in range(4 * g, 4 * g + 4):
+                if k not in dve_planes(j):
+                    nc.scalar.activation(
+                        out=sq_tile(j, g)[:, k % 4, :], in_=zs[j][0][:], func=ACT.Square,
+                        bias=nbias[:, k : k + 1], scale=inv[:, k : k + 1],
+                    )
+
+        def exp_act(j, g):
+            phi = work.tile([P, 4 * PX], BF16, tag="phi", align_bytes=64)
+            nc.scalar.activation(
+                out=phi[:].rearrange("p (c i t) -> p c t i", i=4, t=4),
+                in_=sqs[(j, g)][:].rearrange("p t (c i) -> p c t i", i=4),
+                func=ACT.Exp, scale=-1.0,
+            )
+            phis[(j, g)] = phi
+
+        def quant_phi(j, g):
+            pq = work.tile([P, PX], U32, tag="pq", align_bytes=64)
+            ps = work.tile([P, PX], U8, tag="ps", align_bytes=64)
+            nc.vector.quantize_mx(out=pq[:].bitcast(FP8X4), scales=ps[:], in_=phis[(j, g)][:])
+            pqs[(j, g)] = (pq, ps)
+
+        def mm_out(j, g):
+            pq, ps = pqs[(j, g)]
+            for h in range(2):
+                if g == 0:
+                    ops[(j, h)] = psum.tile([P, PX], F32, tag="o", bufs=4, name="o_ps")
+                nc.tensor.matmul_mx(
+                    out=ops[(j, h)][:],
+                    lhsT=oq[g][:, h * P : (h + 1) * P].bitcast(FP8X4),
+                    lhsT_scale=osc[g][:, h * P : (h + 1) * P],
+                    rhs=pq[:].bitcast(FP8X4), rhs_scale=ps[:], start=(g == 0), stop=(g == 1),
+                )
+
+        def evacuate(j, h, engine):
+            b, w0 = j // 2, (j % 2) * PX
+            o_sb = work.tile([P, PX], F32, tag="o_sb", bufs=6)
+            if engine == "act":
+                nc.scalar.activation(out=o_sb[:], in_=ops[(j, h)][:], func=ACT.Identity, bias=obf[h][:, 0:1], scale=1.0)
+            else:
+                nc.vector.tensor_scalar(out=o_sb[:], in0=ops[(j, h)][:], scalar1=obf[h][:, 0:1], scalar2=None, op0=ALU.add)
+            nc.sync.dma_start(
+                out=out[b, h * P : (h + 1) * P].rearrange("o h w -> o (h w)")[:, w0 : w0 + PX], in_=o_sb[:]
+            )
+
+        wt = psum.tile([P, 2, P], F32, tag="o", bufs=4)
+        w_words = w_sb[:].bitcast(F32).rearrange("c (p u) -> c u p", u=2)
+        for u in range(2):
+            nc.tensor.transpose(out=wt[:, u, :], in_=w_words[:, u, :], identity=ident[:])
+        th = small("th")
+        nc.scalar.activation(out=th[:], in_=lwb[:], func=ACT.Tanh, scale=0.5)
+
+        binf = small("binf", 1)
+        nc.vector.tensor_copy(out=binf[:], in_=binb[:])
+        relu_c = small("relu_c")
+        nc.vector.tensor_scalar(
+            out=relu_c[:], in0=lwb[:], scalar1=0.0, scalar2=math.log(1.6) + 1e-4, op0=ALU.max, op1=ALU.add
+        )
+        nc.vector.tensor_copy(out=obf[0][:], in_=ob0[:])
+        nc.vector.tensor_copy(out=obf[1][:], in_=ob1[:])
+        nc.vector.tensor_scalar(out=shift[:], in0=cenb[:], scalar1=binf[:, 0:1], scalar2=None, op0=ALU.subtract)
+        wg = const.tile([P, 4 * HID], BF16, align_bytes=64)
+        nc.vector.tensor_copy(
+            out=wg[:].bitcast(F32).rearrange("p (c u) -> p c u", u=2), in_=wt[:].rearrange("p u c -> p c u")
+        )
+        ab = small("ab")
+        nc.vector.scalar_tensor_tensor(out=ab[:], in0=th[:], scalar=-1.0, in1=th[:], op0=ALU.mult, op1=ALU.max)
+        den = small("den")
+        nc.vector.tensor_scalar(out=den[:], in0=ab[:], scalar1=4.0, scalar2=9.0, op0=ALU.mult, op1=ALU.add)
+        num = small("num")
+        nc.vector.tensor_scalar(out=num[:], in0=ab[:], scalar1=-4.0, scalar2=1.0, op0=ALU.mult, op1=ALU.add)
+        nc.vector.quantize_mx(out=wq[:].bitcast(FP8X4), scales=ws[:], in_=wg[:])
+        rden = small("rden")
+        nc.vector.reciprocal(out=rden[:], in_=den[:])
+        regroup(0, "dve", 0, 1)
+        s1 = small("s1")
+        nc.vector.tensor_tensor(out=s1[:], in0=num[:], in1=rden[:], op=ALU.mult)
+        regroup(0, "dve", 1, 2)
+        s2 = small("s2")
+        nc.vector.tensor_tensor(out=s2[:], in0=s1[:], in1=s1[:], op=ALU.mult)
+        regroup(0, "dve", 2, 3)
+        acc = small("acc0")
+        nc.vector.tensor_scalar(out=acc[:], in0=s2[:], scalar1=1.0 / 9.0, scalar2=None, op0=ALU.mult)
+        regroup(0, "dve", 3, 4)
+        for n, coef in enumerate((1.0 / 7.0, 1.0 / 5.0, 1.0 / 3.0)):
+            nxt = small("acc%d" % (n + 1))
+            nc.vector.scalar_tensor_tensor(out=nxt[:], in0=acc[:], scalar=coef, in1=s2[:], op0=ALU.add, op1=ALU.mult)
+            acc = nxt
+            if n == 0:
+                quant_x(0)
+                mm_z(0)
+        half_ln = small("half_ln")
+        nc.vector.scalar_tensor_tensor(out=half_ln[:], in0=acc[:], scalar=1.0, in1=s1[:], op0=ALU.add, op1=ALU.mult)
+        wid = small("wid")
+        nc.vector.scalar_tensor_tensor(out=wid[:], in0=half_ln[:], scalar=2.0, in1=relu_c[:], op0=ALU.mult, op1=ALU.add)
+        nc.vector.reciprocal(out=inv[:], in_=wid[:])
+        nc.vector.scalar_tensor_tensor(out=nbias[:], in0=shift[:], scalar=-1.0, in1=inv[:], op0=ALU.mult, op1=ALU.mult)
+
+        regroup(1, "act")
+        ogs = []
+        for g in range(2):
+            ot_ps = psum.tile([P, 2, C_OUT], F32, tag="o", bufs=4)
+            for u in range(2):
+                for h in range(2):
+                    words = ow_sb[h][:].bitcast(F32).rearrange("o (c q) -> o q c", q=4)
+                    nc.tensor.transpose(
+                        out=ot_ps[:, u, h * P : (h + 1) * P], in_=words[:, 2 * g + u, :], identity=ident[:]
+                    )
+            og = const.tile([P, 4 * C_OUT], BF16, name="og%d" % g, align_bytes=64)
+            nc.scalar.copy(
+                out=og[:].bitcast(F32).rearrange("p (m u) -> p m u", u=2), in_=ot_ps[:].rearrange("p u m -> p m u")
+            )
+            ogs.append(og)
+
+        def quant_ow(g):
+            oq_g = const.tile([P, C_OUT], U32, name="oq%d" % g, align_bytes=64)
+            os_g = const.tile([P, C_OUT], U8, name="os%d" % g, align_bytes=64)
+            nc.vector.quantize_mx(out=oq_g[:].bitcast(FP8X4), scales=os_g[:], in_=ogs[g][:])
+            oq.append(oq_g)
+            osc.append(os_g)
+
+        for it in range(NT):
+            late = [k for k in dve_planes(it) if k >= 4]
+            last = it == NT - 1
+            if it >= 1:
+                quant_phi(it - 1, 1)
+                mm_out(it - 1, 1)
+            squares_act(it, 0)
+            square_dve(it, late[0])
+            if last:
+                for k in late[1:]:
+                    square_dve(it, k)
+            if it >= 1:
+                evacuate(it - 1, 0, "dve")
+                evacuate(it - 1, 1, "dve")
+            exp_act(it, 0)
+            if not last:
+                for k in late[1:]:
+                    square_dve(it, k)
+            squares_act(it, 1)
+            if it == 0:
+                quant_ow(0)
+                quant_ow(1)
+                quant_x(1)
+                mm_z(1)
+                regroup(2, "dve")
+            quant_phi(it, 0)
+            mm_out(it, 0)
+            if it + 2 < NT:
+                quant_x(it + 2)
+                mm_z(it + 2)
+            exp_act(it, 1)
+            if it + 1 < NT:
+                for k in dve_planes(it + 1):
+                    if k < 4:
+                        square_dve(it + 1, k)
+            if it + 3 < NT:
+                regroup(it + 3, "dve")
+        quant_phi(NT - 1, 1)
+        mm_out(NT - 1, 1)
+        evacuate(NT - 1, 0, "act")
+        evacuate(NT - 1, 1, "dve")

@@ -22,9 +22,7 @@ FLOPS = 2 * B * HW * (C_IN * HID + HID * K * C_OUT)
 def dve_planes(j):
     if j == 0:
         return (6, 7)
-    if j == NT - 1:
-        return (2, 3, 5, 6, 7)
-    return (3, 6, 7)
+    return (2, 3, 6, 7)
 
 
 def tile_rbfkanhead_t_kernel(tc, x, w_in, b_in, centers, log_widths, out_weight, out_bias, out):
@@ -61,7 +59,9 @@ def tile_rbfkanhead_t_kernel(tc, x, w_in, b_in, centers, log_widths, out_weight,
             t_ow = const.tile([P, HID * K], BF16, name="ow_sb%d" % h)
             nc.sync.dma_start(out=t_ow[:], in_=owv[h * P : (h + 1) * P, :])
             ow_sb.append(t_ow)
-        for b in range(1, B):
+        nc.sync.dma_start(out=xr[1][:, :, 0:PX], in_=xv[1][:, :, 0:PX])
+        nc.sync.dma_start(out=xr[1][:, :, PX:HW], in_=xv[1][:, :, PX:HW])
+        for b in range(2, B):
             nc.sync.dma_start(out=xr[b][:], in_=xv[b])
         ident = const.tile([P, P], F32)
         masks.make_identity(nc, ident[:])
@@ -72,6 +72,10 @@ def tile_rbfkanhead_t_kernel(tc, x, w_in, b_in, centers, log_widths, out_weight,
         shift = small("shift")
         inv = small("inv")
         nbias = small("nbias")
+        negshift = small("negshift")
+        inv2 = small("inv2")
+        zcs = {}
+        vvs = {}
         obf = [small("obf0", 1), small("obf1", 1)]
         wq = const.tile([P, HID], U32, align_bytes=64)
         ws = const.tile([P, HID], U8, align_bytes=64)
@@ -105,27 +109,40 @@ def tile_rbfkanhead_t_kernel(tc, x, w_in, b_in, centers, log_widths, out_weight,
         def mm_z(j):
             xq, xs = xqs[j]
             pair = []
-            for nm in ("zA", "zD"):
+            for nm in ("zD", "zA"):
                 z_ps = psum.tile([P, PX], F32, tag=nm, bufs=2, name=nm)
                 nc.tensor.matmul_mx(
                     out=z_ps[:], lhsT=wq[:].bitcast(FP8X4), lhsT_scale=ws[:],
                     rhs=xq[:].bitcast(FP8X4), rhs_scale=xs[:], start=True, stop=True,
                 )
                 pair.append(z_ps)
-            zs[j] = pair
+            zs[j] = (pair[1], pair[0])
 
         def sq_tile(j, g):
             if (j, g) not in sqs:
                 sqs[(j, g)] = work.tile([P, 4, PX], F32, tag="sq", bufs=4, name="sq")
             return sqs[(j, g)]
 
-        def square_dve(j, k):
-            uu = work.tile([P, PX], F32, tag="uu")
-            nc.vector.tensor_scalar(
-                out=uu[:], in0=zs[j][1][:], scalar1=shift[:, k : k + 1], scalar2=inv[:, k : k + 1],
-                op0=ALU.subtract, op1=ALU.mult,
-            )
-            nc.vector.tensor_tensor(out=sq_tile(j, k // 4)[:, k % 4, :], in0=uu[:], in1=uu[:], op=ALU.mult)
+        def copy_z(j):
+            zc = work.tile([P, PX], F32, tag="zc")
+            nc.vector.tensor_copy(out=zc[:], in_=zs[j][1][:])
+            zcs[j] = zc
+
+        def scaled_gp(j):
+            for k in dve_planes(j):
+                vv = work.tile([P, PX], F32, tag="vv", bufs=8)
+                nc.gpsimd.tensor_scalar(
+                    out=vv[:], in0=zcs[j][:], scalar1=negshift[:, k : k + 1], scalar2=inv2[:, k : k + 1],
+                    op0=ALU.add, op1=ALU.mult,
+                )
+                vvs[(j, k)] = vv
+
+        def squares_dve(j):
+            for k in dve_planes(j):
+                nc.vector.scalar_tensor_tensor(
+                    out=sq_tile(j, k // 4)[:, k % 4, :], in0=zs[j][1][:], scalar=shift[:, k : k + 1],
+                    in1=vvs[(j, k)][:], op0=ALU.subtract, op1=ALU.mult,
+                )
 
         def squares_act(j, g):
             for k in range(4 * g, 4 * g + 4):
@@ -179,55 +196,73 @@ def tile_rbfkanhead_t_kernel(tc, x, w_in, b_in, centers, log_widths, out_weight,
             nc.tensor.transpose(out=wt[:, u, :], in_=w_words[:, u, :], identity=ident[:])
         th = small("th")
         nc.scalar.activation(out=th[:], in_=lwb[:], func=ACT.Tanh, scale=0.5)
+        regroup(1, "act")
+
+        def ts(nm, in0, c1, c2, op0, op1):
+            t_new = small(nm)
+            nc.vector.tensor_scalar(out=t_new[:], in0=in0[:], scalar1=c1, scalar2=c2, op0=op0, op1=op1)
+            return t_new
+
+        def tt(nm, in0, in1):
+            t_new = small(nm)
+            nc.vector.tensor_tensor(out=t_new[:], in0=in0[:], in1=in1[:], op=ALU.mult)
+            return t_new
+
+        def stt(nm, in0, c, in1, op0, op1):
+            t_new = small(nm)
+            nc.vector.scalar_tensor_tensor(out=t_new[:], in0=in0[:], scalar=c, in1=in1[:], op0=op0, op1=op1)
+            return t_new
 
         binf = small("binf", 1)
         nc.vector.tensor_copy(out=binf[:], in_=binb[:])
-        relu_c = small("relu_c")
-        nc.vector.tensor_scalar(
-            out=relu_c[:], in0=lwb[:], scalar1=0.0, scalar2=math.log(1.6) + 1e-4, op0=ALU.max, op1=ALU.add
-        )
+        relu_c = ts("relu_c", lwb, 0.0, math.log(1.6) + 1e-4, ALU.max, ALU.add)
         nc.vector.tensor_copy(out=obf[0][:], in_=ob0[:])
         nc.vector.tensor_copy(out=obf[1][:], in_=ob1[:])
         nc.vector.tensor_scalar(out=shift[:], in0=cenb[:], scalar1=binf[:, 0:1], scalar2=None, op0=ALU.subtract)
+        nc.vector.tensor_scalar(out=negshift[:], in0=shift[:], scalar1=-1.0, scalar2=None, op0=ALU.mult)
         wg = const.tile([P, 4 * HID], BF16, align_bytes=64)
         nc.vector.tensor_copy(
             out=wg[:].bitcast(F32).rearrange("p (c u) -> p c u", u=2), in_=wt[:].rearrange("p u c -> p c u")
         )
-        ab = small("ab")
-        nc.vector.scalar_tensor_tensor(out=ab[:], in0=th[:], scalar=-1.0, in1=th[:], op0=ALU.mult, op1=ALU.max)
-        den = small("den")
-        nc.vector.tensor_scalar(out=den[:], in0=ab[:], scalar1=4.0, scalar2=9.0, op0=ALU.mult, op1=ALU.add)
-        num = small("num")
-        nc.vector.tensor_scalar(out=num[:], in0=ab[:], scalar1=-4.0, scalar2=1.0, op0=ALU.mult, op1=ALU.add)
+        ab = stt("ab", th, -1.0, th, ALU.mult, ALU.max)
+        den = ts("den", ab, 4.0, 9.0, ALU.mult, ALU.add)
+        num = ts("num", ab, -4.0, 1.0, ALU.mult, ALU.add)
         nc.vector.quantize_mx(out=wq[:].bitcast(FP8X4), scales=ws[:], in_=wg[:])
         rden = small("rden")
         nc.vector.reciprocal(out=rden[:], in_=den[:])
         regroup(0, "dve", 0, 1)
-        s1 = small("s1")
-        nc.vector.tensor_tensor(out=s1[:], in0=num[:], in1=rden[:], op=ALU.mult)
+        s1 = tt("s1", num, rden)
         regroup(0, "dve", 1, 2)
-        s2 = small("s2")
-        nc.vector.tensor_tensor(out=s2[:], in0=s1[:], in1=s1[:], op=ALU.mult)
+        s2 = tt("s2", s1, s1)
         regroup(0, "dve", 2, 3)
-        acc = small("acc0")
-        nc.vector.tensor_scalar(out=acc[:], in0=s2[:], scalar1=1.0 / 9.0, scalar2=None, op0=ALU.mult)
+        s4 = tt("s4", s2, s2)
+        p23 = ts("p23", s2, 1.0 / 7.0, 1.0 / 5.0, ALU.mult, ALU.add)
+        p01 = ts("p01", s2, 1.0 / 3.0, 1.0, ALU.mult, ALU.add)
         regroup(0, "dve", 3, 4)
-        for n, coef in enumerate((1.0 / 7.0, 1.0 / 5.0, 1.0 / 3.0)):
-            nxt = small("acc%d" % (n + 1))
-            nc.vector.scalar_tensor_tensor(out=nxt[:], in0=acc[:], scalar=coef, in1=s2[:], op0=ALU.add, op1=ALU.mult)
-            acc = nxt
-            if n == 0:
-                quant_x(0)
-                mm_z(0)
-        half_ln = small("half_ln")
-        nc.vector.scalar_tensor_tensor(out=half_ln[:], in0=acc[:], scalar=1.0, in1=s1[:], op0=ALU.add, op1=ALU.mult)
-        wid = small("wid")
-        nc.vector.scalar_tensor_tensor(out=wid[:], in0=half_ln[:], scalar=2.0, in1=relu_c[:], op0=ALU.mult, op1=ALU.add)
+        t1 = stt("t1", s4, 1.0 / 9.0, p23, ALU.mult, ALU.add)
+        s5 = tt("s5", s4, s1)
+        q01 = tt("q01", p01, s1)
+        quant_x(0)
+        mm_z(0)
+        hi = tt("hi", t1, s5)
+        lo = stt("lo", q01, 2.0, relu_c, ALU.mult, ALU.add)
+        wid = stt("wid", hi, 2.0, lo, ALU.mult, ALU.add)
         nc.vector.reciprocal(out=inv[:], in_=wid[:])
         nc.vector.scalar_tensor_tensor(out=nbias[:], in0=shift[:], scalar=-1.0, in1=inv[:], op0=ALU.mult, op1=ALU.mult)
+        nc.vector.tensor_tensor(out=inv2[:], in0=inv[:], in1=inv[:], op=ALU.mult)
 
-        regroup(1, "act")
+        copy_z(0)
+        scaled_gp(0)
+        quant_x(1)
+        mm_z(1)
+        squares_act(0, 0)
+        regroup(2, "dve")
+        copy_z(1)
+        scaled_gp(1)
+        squares_dve(0)
+
         ogs = []
+        ot_pss = []
         for g in range(2):
             ot_ps = psum.tile([P, 2, C_OUT], F32, tag="o", bufs=4)
             for u in range(2):
@@ -236,9 +271,12 @@ def tile_rbfkanhead_t_kernel(tc, x, w_in, b_in, centers, log_widths, out_weight,
                     nc.tensor.transpose(
                         out=ot_ps[:, u, h * P : (h + 1) * P], in_=words[:, 2 * g + u, :], identity=ident[:]
                     )
+            ot_pss.append(ot_ps)
+
+        def copy_ow(g):
             og = const.tile([P, 4 * C_OUT], BF16, name="og%d" % g, align_bytes=64)
-            nc.scalar.copy(
-                out=og[:].bitcast(F32).rearrange("p (m u) -> p m u", u=2), in_=ot_ps[:].rearrange("p u m -> p m u")
+            nc.vector.tensor_copy(
+                out=og[:].bitcast(F32).rearrange("p (m u) -> p m u", u=2), in_=ot_pss[g][:].rearrange("p u m -> p m u")
             )
             ogs.append(og)
 
@@ -250,42 +288,34 @@ def tile_rbfkanhead_t_kernel(tc, x, w_in, b_in, centers, log_widths, out_weight,
             osc.append(os_g)
 
         for it in range(NT):
-            late = [k for k in dve_planes(it) if k >= 4]
-            last = it == NT - 1
-            if it >= 1:
-                quant_phi(it - 1, 1)
-                mm_out(it - 1, 1)
-            squares_act(it, 0)
-            square_dve(it, late[0])
-            if last:
-                for k in late[1:]:
-                    square_dve(it, k)
-            if it >= 1:
-                evacuate(it - 1, 0, "dve")
-                evacuate(it - 1, 1, "dve")
-            exp_act(it, 0)
-            if not last:
-                for k in late[1:]:
-                    square_dve(it, k)
             squares_act(it, 1)
-            if it == 0:
-                quant_ow(0)
-                quant_ow(1)
-                quant_x(1)
-                mm_z(1)
-                regroup(2, "dve")
-            quant_phi(it, 0)
-            mm_out(it, 0)
             if it + 2 < NT:
                 quant_x(it + 2)
                 mm_z(it + 2)
-            exp_act(it, 1)
-            if it + 1 < NT:
-                for k in dve_planes(it + 1):
-                    if k < 4:
-                        square_dve(it + 1, k)
             if it + 3 < NT:
                 regroup(it + 3, "dve")
+            if it >= 1:
+                quant_phi(it - 1, 1)
+                mm_out(it - 1, 1)
+            else:
+                copy_ow(0)
+                copy_ow(1)
+            exp_act(it, 0)
+            if it + 2 < NT:
+                copy_z(it + 2)
+                scaled_gp(it + 2)
+            if it + 1 < NT:
+                squares_dve(it + 1)
+                squares_act(it + 1, 0)
+            if it >= 1:
+                evacuate(it - 1, 0, "dve")
+                evacuate(it - 1, 1, "dve")
+            else:
+                quant_ow(0)
+                quant_ow(1)
+            exp_act(it, 1)
+            quant_phi(it, 0)
+            mm_out(it, 0)
         quant_phi(NT - 1, 1)
         mm_out(NT - 1, 1)
         evacuate(NT - 1, 0, "act")

@@ -15,8 +15,10 @@ ALU = mybir.AluOpType
 B, C_IN, HW, HID, K, C_OUT = 8, 512, 1024, 128, 8, 256
 P = 128
 PX = 512
-NT = B * HW // PX
 FLOPS = 2 * B * HW * (C_IN * HID + HID * K * C_OUT)
+
+TILES = [(b, w0, PX) for b in range(B) for w0 in (0, PX)][:-1] + [(B - 1, PX, PX // 2), (B - 1, PX + PX // 2, PX // 2)]
+NT = len(TILES)
 
 
 def dve_planes(j):
@@ -40,9 +42,9 @@ def tile_rbfkanhead_t_kernel(tc, x, w_in, b_in, centers, log_widths, out_weight,
         ob0 = const.tile([P, 1], BF16)
         ob1 = const.tile([P, 1], BF16)
         with nc.allow_non_contiguous_dma(reason="small per-channel tables"):
-            nc.scalar.dma_start(out=lwb[:], in_=log_widths.rearrange("a c k x y -> (a c) (k x y)"))
-            nc.scalar.dma_start(out=cenb[:], in_=centers.rearrange("a c k x y -> (a c) (k x y)"))
-            nc.scalar.dma_start(out=binb[:], in_=b_in.rearrange("(c o) -> c o", o=1))
+            nc.sync.dma_start(out=lwb[:], in_=log_widths.rearrange("a c k x y -> (a c) (k x y)"))
+            nc.sync.dma_start(out=cenb[:], in_=centers.rearrange("a c k x y -> (a c) (k x y)"))
+            nc.sync.dma_start(out=binb[:], in_=b_in.rearrange("(c o) -> c o", o=1))
             nc.scalar.dma_start(out=ob0[:], in_=out_bias[0:P].rearrange("(c o) -> c o", o=1))
             nc.scalar.dma_start(out=ob1[:], in_=out_bias[P : 2 * P].rearrange("(c o) -> c o", o=1))
         w_sb = const.tile([P, C_IN], BF16)
@@ -51,16 +53,15 @@ def tile_rbfkanhead_t_kernel(tc, x, w_in, b_in, centers, log_widths, out_weight,
         for b in range(B):
             xr.append(xin.tile([P, 4, HW], BF16, name="xr%d" % b))
         xv = [x[b].rearrange("(p j) h w -> p j (h w)", j=4) for b in range(B)]
-        nc.sync.dma_start(out=xr[0][:, :, 0:PX], in_=xv[0][:, :, 0:PX])
-        nc.sync.dma_start(out=xr[0][:, :, PX:HW], in_=xv[0][:, :, PX:HW])
+        for b in range(2):
+            nc.sync.dma_start(out=xr[b][:, :, 0:PX], in_=xv[b][:, :, 0:PX])
+            nc.sync.dma_start(out=xr[b][:, :, PX:HW], in_=xv[b][:, :, PX:HW])
         ow_sb = []
         owv = out_weight.rearrange("o c k -> o (c k)")
         for h in range(2):
             t_ow = const.tile([P, HID * K], BF16, name="ow_sb%d" % h)
             nc.sync.dma_start(out=t_ow[:], in_=owv[h * P : (h + 1) * P, :])
             ow_sb.append(t_ow)
-        nc.sync.dma_start(out=xr[1][:, :, 0:PX], in_=xv[1][:, :, 0:PX])
-        nc.sync.dma_start(out=xr[1][:, :, PX:HW], in_=xv[1][:, :, PX:HW])
         for b in range(2, B):
             nc.sync.dma_start(out=xr[b][:], in_=xv[b])
         ident = const.tile([P, P], F32)
@@ -74,8 +75,6 @@ def tile_rbfkanhead_t_kernel(tc, x, w_in, b_in, centers, log_widths, out_weight,
         nbias = small("nbias")
         negshift = small("negshift")
         inv2 = small("inv2")
-        zcs = {}
-        vvs = {}
         obf = [small("obf0", 1), small("obf1", 1)]
         wq = const.tile([P, HID], U32, align_bytes=64)
         ws = const.tile([P, HID], U8, align_bytes=64)
@@ -84,15 +83,19 @@ def tile_rbfkanhead_t_kernel(tc, x, w_in, b_in, centers, log_widths, out_weight,
         xgs = {}
         xqs = {}
         zs = {}
+        zcs = {}
+        vvs = {}
         sqs = {}
         phis = {}
         pqs = {}
         ops = {}
 
-        def regroup(j, engine, q0=0, q1=4):
-            b, w0 = j // 2, (j % 2) * PX
+        def regroup(j, engine, q0=0, q1=None):
+            b, w0, n = TILES[j]
+            if q1 is None:
+                q1 = n // 128
             if j not in xgs:
-                xgs[j] = work.tile([P, 4 * PX], BF16, tag="xg", name="xg", align_bytes=64)
+                xgs[j] = work.tile([P, 4 * n], BF16, tag="xg", name="xg", align_bytes=64)
             dst = xgs[j][:, 512 * q0 : 512 * q1].rearrange("p (c i t) -> p c t i", i=4, t=4)
             src = xr[b][:, :, w0 + 128 * q0 : w0 + 128 * q1].rearrange("p t (c i) -> p c t i", i=4)
             if engine == "act":
@@ -101,36 +104,37 @@ def tile_rbfkanhead_t_kernel(tc, x, w_in, b_in, centers, log_widths, out_weight,
                 nc.vector.tensor_copy(out=dst, in_=src)
 
         def quant_x(j):
-            xq = work.tile([P, PX], U32, tag="xq", align_bytes=64)
-            xs = work.tile([P, PX], U8, tag="xs", align_bytes=64)
+            n = TILES[j][2]
+            xq = work.tile([P, n], U32, tag="xq", align_bytes=64)
+            xs = work.tile([P, n], U8, tag="xs", align_bytes=64)
             nc.vector.quantize_mx(out=xq[:].bitcast(FP8X4), scales=xs[:], in_=xgs[j][:])
             xqs[j] = (xq, xs)
 
         def mm_z(j):
             xq, xs = xqs[j]
-            pair = []
-            for nm in ("zD", "zA"):
-                z_ps = psum.tile([P, PX], F32, tag=nm, bufs=2, name=nm)
-                nc.tensor.matmul_mx(
-                    out=z_ps[:], lhsT=wq[:].bitcast(FP8X4), lhsT_scale=ws[:],
-                    rhs=xq[:].bitcast(FP8X4), rhs_scale=xs[:], start=True, stop=True,
-                )
-                pair.append(z_ps)
-            zs[j] = (pair[1], pair[0])
+            z_ps = psum.tile([P, TILES[j][2]], F32, tag="z", bufs=3)
+            nc.tensor.matmul_mx(
+                out=z_ps[:], lhsT=wq[:].bitcast(FP8X4), lhsT_scale=ws[:],
+                rhs=xq[:].bitcast(FP8X4), rhs_scale=xs[:], start=True, stop=True,
+            )
+            zs[j] = z_ps
+
+        def copy_z(j, engine):
+            zc = work.tile([P, TILES[j][2]], F32, tag="zc", bufs=4)
+            if engine == "act":
+                nc.scalar.copy(out=zc[:], in_=zs[j][:])
+            else:
+                nc.vector.tensor_copy(out=zc[:], in_=zs[j][:])
+            zcs[j] = zc
 
         def sq_tile(j, g):
             if (j, g) not in sqs:
-                sqs[(j, g)] = work.tile([P, 4, PX], F32, tag="sq", bufs=4, name="sq")
+                sqs[(j, g)] = work.tile([P, 4, TILES[j][2]], F32, tag="sq", bufs=5, name="sq")
             return sqs[(j, g)]
-
-        def copy_z(j):
-            zc = work.tile([P, PX], F32, tag="zc")
-            nc.vector.tensor_copy(out=zc[:], in_=zs[j][1][:])
-            zcs[j] = zc
 
         def scaled_gp(j):
             for k in dve_planes(j):
-                vv = work.tile([P, PX], F32, tag="vv", bufs=8)
+                vv = work.tile([P, TILES[j][2]], F32, tag="vv", bufs=8)
                 nc.gpsimd.tensor_scalar(
                     out=vv[:], in0=zcs[j][:], scalar1=negshift[:, k : k + 1], scalar2=inv2[:, k : k + 1],
                     op0=ALU.add, op1=ALU.mult,
@@ -140,7 +144,7 @@ def tile_rbfkanhead_t_kernel(tc, x, w_in, b_in, centers, log_widths, out_weight,
         def squares_dve(j):
             for k in dve_planes(j):
                 nc.vector.scalar_tensor_tensor(
-                    out=sq_tile(j, k // 4)[:, k % 4, :], in0=zs[j][1][:], scalar=shift[:, k : k + 1],
+                    out=sq_tile(j, k // 4)[:, k % 4, :], in0=zs[j][:], scalar=shift[:, k : k + 1],
                     in1=vvs[(j, k)][:], op0=ALU.subtract, op1=ALU.mult,
                 )
 
@@ -148,12 +152,12 @@ def tile_rbfkanhead_t_kernel(tc, x, w_in, b_in, centers, log_widths, out_weight,
             for k in range(4 * g, 4 * g + 4):
                 if k not in dve_planes(j):
                     nc.scalar.activation(
-                        out=sq_tile(j, g)[:, k % 4, :], in_=zs[j][0][:], func=ACT.Square,
+                        out=sq_tile(j, g)[:, k % 4, :], in_=zcs[j][:], func=ACT.Square,
                         bias=nbias[:, k : k + 1], scale=inv[:, k : k + 1],
                     )
 
         def exp_act(j, g):
-            phi = work.tile([P, 4 * PX], BF16, tag="phi", align_bytes=64)
+            phi = work.tile([P, 4 * TILES[j][2]], BF16, tag="phi", align_bytes=64)
             nc.scalar.activation(
                 out=phi[:].rearrange("p (c i t) -> p c t i", i=4, t=4),
                 in_=sqs[(j, g)][:].rearrange("p t (c i) -> p c t i", i=4),
@@ -162,8 +166,9 @@ def tile_rbfkanhead_t_kernel(tc, x, w_in, b_in, centers, log_widths, out_weight,
             phis[(j, g)] = phi
 
         def quant_phi(j, g):
-            pq = work.tile([P, PX], U32, tag="pq", align_bytes=64)
-            ps = work.tile([P, PX], U8, tag="ps", align_bytes=64)
+            n = TILES[j][2]
+            pq = work.tile([P, n], U32, tag="pq", align_bytes=64)
+            ps = work.tile([P, n], U8, tag="ps", align_bytes=64)
             nc.vector.quantize_mx(out=pq[:].bitcast(FP8X4), scales=ps[:], in_=phis[(j, g)][:])
             pqs[(j, g)] = (pq, ps)
 
@@ -171,7 +176,7 @@ def tile_rbfkanhead_t_kernel(tc, x, w_in, b_in, centers, log_widths, out_weight,
             pq, ps = pqs[(j, g)]
             for h in range(2):
                 if g == 0:
-                    ops[(j, h)] = psum.tile([P, PX], F32, tag="o", bufs=4, name="o_ps")
+                    ops[(j, h)] = psum.tile([P, TILES[j][2]], F32, tag="o", bufs=4, name="o_ps")
                 nc.tensor.matmul_mx(
                     out=ops[(j, h)][:],
                     lhsT=oq[g][:, h * P : (h + 1) * P].bitcast(FP8X4),
@@ -180,14 +185,14 @@ def tile_rbfkanhead_t_kernel(tc, x, w_in, b_in, centers, log_widths, out_weight,
                 )
 
         def evacuate(j, h, engine):
-            b, w0 = j // 2, (j % 2) * PX
-            o_sb = work.tile([P, PX], F32, tag="o_sb", bufs=6)
+            b, w0, n = TILES[j]
+            o_sb = work.tile([P, n], F32, tag="o_sb", bufs=6)
             if engine == "act":
                 nc.scalar.activation(out=o_sb[:], in_=ops[(j, h)][:], func=ACT.Identity, bias=obf[h][:, 0:1], scale=1.0)
             else:
                 nc.vector.tensor_scalar(out=o_sb[:], in0=ops[(j, h)][:], scalar1=obf[h][:, 0:1], scalar2=None, op0=ALU.add)
             nc.sync.dma_start(
-                out=out[b, h * P : (h + 1) * P].rearrange("o h w -> o (h w)")[:, w0 : w0 + PX], in_=o_sb[:]
+                out=out[b, h * P : (h + 1) * P].rearrange("o h w -> o (h w)")[:, w0 : w0 + n], in_=o_sb[:]
             )
 
         wt = psum.tile([P, 2, P], F32, tag="o", bufs=4)
@@ -244,6 +249,7 @@ def tile_rbfkanhead_t_kernel(tc, x, w_in, b_in, centers, log_widths, out_weight,
         q01 = tt("q01", p01, s1)
         quant_x(0)
         mm_z(0)
+        copy_z(0, "act")
         hi = tt("hi", t1, s5)
         lo = stt("lo", q01, 2.0, relu_c, ALU.mult, ALU.add)
         wid = stt("wid", hi, 2.0, lo, ALU.mult, ALU.add)
@@ -251,13 +257,12 @@ def tile_rbfkanhead_t_kernel(tc, x, w_in, b_in, centers, log_widths, out_weight,
         nc.vector.scalar_tensor_tensor(out=nbias[:], in0=shift[:], scalar=-1.0, in1=inv[:], op0=ALU.mult, op1=ALU.mult)
         nc.vector.tensor_tensor(out=inv2[:], in0=inv[:], in1=inv[:], op=ALU.mult)
 
-        copy_z(0)
         scaled_gp(0)
         quant_x(1)
         mm_z(1)
         squares_act(0, 0)
         regroup(2, "dve")
-        copy_z(1)
+        copy_z(1, "dve")
         scaled_gp(1)
         squares_dve(0)
 
@@ -302,11 +307,14 @@ def tile_rbfkanhead_t_kernel(tc, x, w_in, b_in, centers, log_widths, out_weight,
                 copy_ow(1)
             exp_act(it, 0)
             if it + 2 < NT:
-                copy_z(it + 2)
+                copy_z(it + 2, "dve")
                 scaled_gp(it + 2)
             if it + 1 < NT:
                 squares_dve(it + 1)
                 squares_act(it + 1, 0)
+            if it + 2 >= NT:
+                quant_phi(it, 0)
+                mm_out(it, 0)
             if it >= 1:
                 evacuate(it - 1, 0, "dve")
                 evacuate(it - 1, 1, "dve")
@@ -314,8 +322,9 @@ def tile_rbfkanhead_t_kernel(tc, x, w_in, b_in, centers, log_widths, out_weight,
                 quant_ow(0)
                 quant_ow(1)
             exp_act(it, 1)
-            quant_phi(it, 0)
-            mm_out(it, 0)
+            if it + 2 < NT:
+                quant_phi(it, 0)
+                mm_out(it, 0)
         quant_phi(NT - 1, 1)
         mm_out(NT - 1, 1)
         evacuate(NT - 1, 0, "act")

@@ -129,8 +129,14 @@ def tile_rbfkanhead_t_kernel(tc, x, w_in, b_in, centers, log_widths, out_weight,
 
         def sq_tile(j, g):
             if (j, g) not in sqs:
-                sqs[(j, g)] = work.tile([P, 4, TILES[j][2]], F32, tag="sq", bufs=5, name="sq")
+                sqs[(j, g)] = work.tile([P, 4 * TILES[j][2]], F32, tag="sq", bufs=5, name="sq")
             return sqs[(j, g)]
+
+        def plane(j, k):
+            return sq_tile(j, k // 4)[:].rearrange("p (c t i) -> p t c i", t=4, i=4)[:, k % 4]
+
+        def by4(ap):
+            return ap.rearrange("p (c i) -> p c i", i=4)
 
         def scaled_gp(j):
             for k in dve_planes(j):
@@ -144,15 +150,15 @@ def tile_rbfkanhead_t_kernel(tc, x, w_in, b_in, centers, log_widths, out_weight,
         def squares_dve(j):
             for k in dve_planes(j):
                 nc.vector.scalar_tensor_tensor(
-                    out=sq_tile(j, k // 4)[:, k % 4, :], in0=zs[j][:], scalar=shift[:, k : k + 1],
-                    in1=vvs[(j, k)][:], op0=ALU.subtract, op1=ALU.mult,
+                    out=plane(j, k), in0=by4(zs[j][:]), scalar=shift[:, k : k + 1],
+                    in1=by4(vvs[(j, k)][:]), op0=ALU.subtract, op1=ALU.mult,
                 )
 
         def squares_act(j, g):
             for k in range(4 * g, 4 * g + 4):
                 if k not in dve_planes(j):
                     nc.scalar.activation(
-                        out=sq_tile(j, g)[:, k % 4, :], in_=zcs[j][:], func=ACT.Square,
+                        out=plane(j, k), in_=by4(zcs[j][:]), func=ACT.Square,
                         bias=nbias[:, k : k + 1], scale=inv[:, k : k + 1],
                     )
 
@@ -160,7 +166,7 @@ def tile_rbfkanhead_t_kernel(tc, x, w_in, b_in, centers, log_widths, out_weight,
             phi = work.tile([P, 4 * TILES[j][2]], BF16, tag="phi", align_bytes=64)
             nc.scalar.activation(
                 out=phi[:].rearrange("p (c i t) -> p c t i", i=4, t=4),
-                in_=sqs[(j, g)][:].rearrange("p t (c i) -> p c t i", i=4),
+                in_=sqs[(j, g)][:].rearrange("p (c t i) -> p c t i", t=4, i=4),
                 func=ACT.Exp, scale=-1.0,
             )
             phis[(j, g)] = phi

@@ -133,10 +133,8 @@ def tile_rbfkanhead_t_kernel(tc, x, w_in, b_in, centers, log_widths, out_weight,
             return sqs[(j, g)]
 
         def plane(j, k):
-            return sq_tile(j, k // 4)[:].rearrange("p (c t i) -> p t c i", t=4, i=4)[:, k % 4]
-
-        def by4(ap):
-            return ap.rearrange("p (c i) -> p c i", i=4)
+            n = TILES[j][2]
+            return sq_tile(j, k // 4)[:, (k % 4) * n : (k % 4 + 1) * n]
 
         def scaled_gp(j):
             for k in dve_planes(j):
@@ -150,23 +148,23 @@ def tile_rbfkanhead_t_kernel(tc, x, w_in, b_in, centers, log_widths, out_weight,
         def squares_dve(j):
             for k in dve_planes(j):
                 nc.vector.scalar_tensor_tensor(
-                    out=plane(j, k), in0=by4(zs[j][:]), scalar=shift[:, k : k + 1],
-                    in1=by4(vvs[(j, k)][:]), op0=ALU.subtract, op1=ALU.mult,
+                    out=plane(j, k), in0=zs[j][:], scalar=shift[:, k : k + 1],
+                    in1=vvs[(j, k)][:], op0=ALU.subtract, op1=ALU.mult,
                 )
 
         def squares_act(j, g):
             for k in range(4 * g, 4 * g + 4):
                 if k not in dve_planes(j):
                     nc.scalar.activation(
-                        out=plane(j, k), in_=by4(zcs[j][:]), func=ACT.Square,
+                        out=plane(j, k), in_=zcs[j][:], func=ACT.Square,
                         bias=nbias[:, k : k + 1], scale=inv[:, k : k + 1],
                     )
 
         def exp_act(j, g):
             phi = work.tile([P, 4 * TILES[j][2]], BF16, tag="phi", align_bytes=64)
             nc.scalar.activation(
-                out=phi[:].rearrange("p (c i t) -> p c t i", i=4, t=4),
-                in_=sqs[(j, g)][:].rearrange("p (c t i) -> p c t i", t=4, i=4),
+                out=phi[:].rearrange("p (c i t) -> p c t i", i=2, t=4),
+                in_=sqs[(j, g)][:].rearrange("p (t c i) -> p c t i", t=4, i=2),
                 func=ACT.Exp, scale=-1.0,
             )
             phis[(j, g)] = phi

@@ -1,4 +1,3 @@
-import math
 from contextlib import ExitStack
 
 import concourse.masks as masks
@@ -19,12 +18,21 @@ FLOPS = 2 * B * HW * (C_IN * HID + HID * K * C_OUT)
 
 TILES = [(b, w0, PX) for b in range(B) for w0 in (0, PX)][:-1] + [(B - 1, PX, PX // 2), (B - 1, PX + PX // 2, PX // 2)]
 NT = len(TILES)
+R = 2
 
 
 def dve_planes(j):
     if j == 0:
         return (6, 7)
-    return (2, 3, 6, 7)
+    if j >= NT - 2:
+        return (R, 3, 5, 6, 7)
+    return (R, 3, 5, 6, 7) if j % 4 == 0 else (R, 3, 6, 7)
+
+
+def gp_blocks(j):
+    if j < 5 or TILES[j][2] < PX:
+        return 0
+    return 1
 
 
 def tile_rbfkanhead_t_kernel(tc, x, w_in, b_in, centers, log_widths, out_weight, out_bias, out):
@@ -39,23 +47,28 @@ def tile_rbfkanhead_t_kernel(tc, x, w_in, b_in, centers, log_widths, out_weight,
         lwb = const.tile([P, K], BF16)
         cenb = const.tile([P, K], BF16)
         binb = const.tile([P, 1], BF16)
-        ob0 = const.tile([P, 1], BF16)
-        ob1 = const.tile([P, 1], BF16)
-        with nc.allow_non_contiguous_dma(reason="small per-channel tables"):
-            nc.sync.dma_start(out=lwb[:], in_=log_widths.rearrange("a c k x y -> (a c) (k x y)"))
-            nc.sync.dma_start(out=cenb[:], in_=centers.rearrange("a c k x y -> (a c) (k x y)"))
-            nc.sync.dma_start(out=binb[:], in_=b_in.rearrange("(c o) -> c o", o=1))
-            nc.scalar.dma_start(out=ob0[:], in_=out_bias[0:P].rearrange("(c o) -> c o", o=1))
-            nc.scalar.dma_start(out=ob1[:], in_=out_bias[P : 2 * P].rearrange("(c o) -> c o", o=1))
+        obb = [const.tile([P, 1], BF16, name="ob%d" % h) for h in range(2)]
         w_sb = const.tile([P, C_IN], BF16)
-        nc.sync.dma_start(out=w_sb[:], in_=w_in)
         xr = []
         for b in range(B):
             xr.append(xin.tile([P, 4, HW], BF16, name="xr%d" % b))
         xv = [x[b].rearrange("(p j) h w -> p j (h w)", j=4) for b in range(B)]
-        for b in range(2):
-            nc.sync.dma_start(out=xr[b][:, :, 0:PX], in_=xv[b][:, :, 0:PX])
-            nc.sync.dma_start(out=xr[b][:, :, PX:HW], in_=xv[b][:, :, PX:HW])
+
+        def load_x(b, lo, hi):
+            nc.sync.dma_start(out=xr[b][:, :, lo:hi], in_=xv[b][:, :, lo:hi])
+
+        with nc.allow_non_contiguous_dma(reason="small per-channel tables"):
+            nc.sync.dma_start(out=lwb[:], in_=log_widths.rearrange("a c k x y -> (a c) (k x y)"))
+            load_x(0, 0, PX // 2)
+            nc.sync.dma_start(out=w_sb[:], in_=w_in)
+            load_x(0, PX // 2, PX)
+            nc.sync.dma_start(out=cenb[:], in_=centers.rearrange("a c k x y -> (a c) (k x y)"))
+            nc.sync.dma_start(out=binb[:], in_=b_in.rearrange("(c o) -> c o", o=1))
+            for h in range(2):
+                nc.scalar.dma_start(out=obb[h][:], in_=out_bias[h * P : (h + 1) * P].rearrange("(c o) -> c o", o=1))
+        load_x(0, PX, HW)
+        load_x(1, 0, PX)
+        load_x(1, PX, HW)
         ow_sb = []
         owv = out_weight.rearrange("o c k -> o (c k)")
         for h in range(2):
@@ -63,19 +76,13 @@ def tile_rbfkanhead_t_kernel(tc, x, w_in, b_in, centers, log_widths, out_weight,
             nc.sync.dma_start(out=t_ow[:], in_=owv[h * P : (h + 1) * P, :])
             ow_sb.append(t_ow)
         for b in range(2, B):
-            nc.sync.dma_start(out=xr[b][:], in_=xv[b])
+            load_x(b, 0, HW)
         ident = const.tile([P, P], F32)
         masks.make_identity(nc, ident[:])
 
         def small(nm, cols=K):
             return const.tile([P, cols], F32, name=nm)
 
-        shift = small("shift")
-        inv = small("inv")
-        nbias = small("nbias")
-        negshift = small("negshift")
-        inv2 = small("inv2")
-        obf = [small("obf0", 1), small("obf1", 1)]
         wq = const.tile([P, HID], U32, align_bytes=64)
         ws = const.tile([P, HID], U8, align_bytes=64)
         oq = []
@@ -83,7 +90,7 @@ def tile_rbfkanhead_t_kernel(tc, x, w_in, b_in, centers, log_widths, out_weight,
         xgs = {}
         xqs = {}
         zs = {}
-        zcs = {}
+        ys = {}
         vvs = {}
         sqs = {}
         phis = {}
@@ -95,9 +102,17 @@ def tile_rbfkanhead_t_kernel(tc, x, w_in, b_in, centers, log_widths, out_weight,
             if q1 is None:
                 q1 = n // 128
             if j not in xgs:
-                xgs[j] = work.tile([P, 4 * n], BF16, tag="xg", name="xg", align_bytes=64)
-            dst = xgs[j][:, 512 * q0 : 512 * q1].rearrange("p (c i t) -> p c t i", i=4, t=4)
-            src = xr[b][:, :, w0 + 128 * q0 : w0 + 128 * q1].rearrange("p t (c i) -> p c t i", i=4)
+                xgs[j] = work.tile([P, 4 * n], BF16, tag="xg", name="xg", bufs=4, align_bytes=64)
+            dst = xgs[j][:, 512 * q0 : 512 * q1]
+            src = xr[b][:, :, w0 + 128 * q0 : w0 + 128 * q1]
+            if engine == "gp":
+                nc.gpsimd.tensor_scalar(
+                    out=dst.rearrange("p (c t) -> p c t", t=4), in0=src.rearrange("p t c -> p c t"),
+                    scalar1=1.0, scalar2=0.0, op0=ALU.mult, op1=ALU.add,
+                )
+                return
+            dst = dst.rearrange("p (c i t) -> p c t i", i=4, t=4)
+            src = src.rearrange("p t (c i) -> p c t i", i=4)
             if engine == "act":
                 nc.scalar.copy(out=dst, in_=src)
             else:
@@ -119,45 +134,46 @@ def tile_rbfkanhead_t_kernel(tc, x, w_in, b_in, centers, log_widths, out_weight,
             )
             zs[j] = z_ps
 
-        def copy_z(j, engine):
-            zc = work.tile([P, TILES[j][2]], F32, tag="zc", bufs=4)
-            if engine == "act":
-                nc.scalar.copy(out=zc[:], in_=zs[j][:])
-            else:
-                nc.vector.tensor_copy(out=zc[:], in_=zs[j][:])
-            zcs[j] = zc
-
-        def sq_tile(j, g):
-            if (j, g) not in sqs:
-                sqs[(j, g)] = work.tile([P, 4 * TILES[j][2]], F32, tag="sq", bufs=5, name="sq")
-            return sqs[(j, g)]
+        def copy_y(j):
+            y = work.tile([P, TILES[j][2]], F32, tag="y", bufs=4)
+            nc.vector.tensor_scalar(
+                out=y[:], in0=zs[j][:], scalar1=shift[:, R : R + 1], scalar2=inv2[:, R : R + 1],
+                op0=ALU.subtract, op1=ALU.mult,
+            )
+            ys[j] = y
 
         def plane(j, k):
             n = TILES[j][2]
-            return sq_tile(j, k // 4)[:, (k % 4) * n : (k % 4 + 1) * n]
+            g = k // 4
+            if (j, g) not in sqs:
+                sqs[(j, g)] = work.tile([P, 4 * n], F32, tag="sq", bufs=5, name="sq")
+            return sqs[(j, g)][:, (k % 4) * n : (k % 4 + 1) * n]
 
-        def scaled_gp(j):
+        def factors_gp(j):
             for k in dve_planes(j):
-                vv = work.tile([P, TILES[j][2]], F32, tag="vv", bufs=8)
+                if k == R:
+                    continue
+                vv = work.tile([P, TILES[j][2]], F32, tag="vv", bufs=9)
                 nc.gpsimd.tensor_scalar(
-                    out=vv[:], in0=zcs[j][:], scalar1=negshift[:, k : k + 1], scalar2=inv2[:, k : k + 1],
-                    op0=ALU.add, op1=ALU.mult,
+                    out=vv[:], in0=ys[j][:], scalar1=va[:, k : k + 1], scalar2=vb[:, k : k + 1],
+                    op0=ALU.mult, op1=ALU.add,
                 )
                 vvs[(j, k)] = vv
 
         def squares_dve(j):
             for k in dve_planes(j):
+                factor = ys[j] if k == R else vvs[(j, k)]
                 nc.vector.scalar_tensor_tensor(
                     out=plane(j, k), in0=zs[j][:], scalar=shift[:, k : k + 1],
-                    in1=vvs[(j, k)][:], op0=ALU.subtract, op1=ALU.mult,
+                    in1=factor[:], op0=ALU.subtract, op1=ALU.mult,
                 )
 
         def squares_act(j, g):
             for k in range(4 * g, 4 * g + 4):
                 if k not in dve_planes(j):
                     nc.scalar.activation(
-                        out=plane(j, k), in_=zcs[j][:], func=ACT.Square,
-                        bias=nbias[:, k : k + 1], scale=inv[:, k : k + 1],
+                        out=plane(j, k), in_=ys[j][:], func=ACT.Square,
+                        bias=ub[:, k : k + 1], scale=ua[:, k : k + 1],
                     )
 
         def exp_act(j, g):
@@ -192,9 +208,9 @@ def tile_rbfkanhead_t_kernel(tc, x, w_in, b_in, centers, log_widths, out_weight,
             b, w0, n = TILES[j]
             o_sb = work.tile([P, n], F32, tag="o_sb", bufs=6)
             if engine == "act":
-                nc.scalar.activation(out=o_sb[:], in_=ops[(j, h)][:], func=ACT.Identity, bias=obf[h][:, 0:1], scale=1.0)
+                nc.scalar.activation(out=o_sb[:], in_=ops[(j, h)][:], func=ACT.Identity, bias=obb[h][:, 0:1], scale=1.0)
             else:
-                nc.vector.tensor_scalar(out=o_sb[:], in0=ops[(j, h)][:], scalar1=obf[h][:, 0:1], scalar2=None, op0=ALU.add)
+                nc.vector.tensor_scalar(out=o_sb[:], in0=ops[(j, h)][:], scalar1=obb[h][:, 0:1], scalar2=None, op0=ALU.add)
             nc.sync.dma_start(
                 out=out[b, h * P : (h + 1) * P].rearrange("o h w -> o (h w)")[:, w0 : w0 + n], in_=o_sb[:]
             )
@@ -203,71 +219,67 @@ def tile_rbfkanhead_t_kernel(tc, x, w_in, b_in, centers, log_widths, out_weight,
         w_words = w_sb[:].bitcast(F32).rearrange("c (p u) -> c u p", u=2)
         for u in range(2):
             nc.tensor.transpose(out=wt[:, u, :], in_=w_words[:, u, :], identity=ident[:])
-        th = small("th")
-        nc.scalar.activation(out=th[:], in_=lwb[:], func=ACT.Tanh, scale=0.5)
-        regroup(1, "act")
 
         def ts(nm, in0, c1, c2, op0, op1):
             t_new = small(nm)
-            nc.vector.tensor_scalar(out=t_new[:], in0=in0[:], scalar1=c1, scalar2=c2, op0=op0, op1=op1)
+            nc.vector.tensor_scalar(out=t_new[:], in0=in0, scalar1=c1, scalar2=c2, op0=op0, op1=op1)
             return t_new
 
-        def tt(nm, in0, in1):
-            t_new = small(nm)
-            nc.vector.tensor_tensor(out=t_new[:], in0=in0[:], in1=in1[:], op=ALU.mult)
+        def tt(nm, in0, in1, op, cols=K):
+            t_new = small(nm, cols)
+            nc.vector.tensor_tensor(out=t_new[:], in0=in0, in1=in1, op=op)
             return t_new
 
-        def stt(nm, in0, c, in1, op0, op1):
-            t_new = small(nm)
-            nc.vector.scalar_tensor_tensor(out=t_new[:], in0=in0[:], scalar=c, in1=in1[:], op0=op0, op1=op1)
-            return t_new
-
-        binf = small("binf", 1)
-        nc.vector.tensor_copy(out=binf[:], in_=binb[:])
-        relu_c = ts("relu_c", lwb, 0.0, math.log(1.6) + 1e-4, ALU.max, ALU.add)
-        nc.vector.tensor_copy(out=obf[0][:], in_=ob0[:])
-        nc.vector.tensor_copy(out=obf[1][:], in_=ob1[:])
-        nc.vector.tensor_scalar(out=shift[:], in0=cenb[:], scalar1=binf[:, 0:1], scalar2=None, op0=ALU.subtract)
-        nc.vector.tensor_scalar(out=negshift[:], in0=shift[:], scalar1=-1.0, scalar2=None, op0=ALU.mult)
+        mag = small("mag")
+        nc.scalar.activation(out=mag[:], in_=lwb[:], func=ACT.Abs)
+        ex = small("ex")
+        nc.scalar.activation(out=ex[:], in_=mag[:], func=ACT.Exp, scale=-1.0)
+        lg = small("lg")
+        nc.scalar.activation(out=lg[:], in_=ex[:], func=ACT.Ln, bias=1.0, scale=1.0)
+        warm = small("warm")
+        nc.scalar.activation(out=warm[:], in_=mag[:], func=ACT.Exp, scale=-1.0)
+        relu_c = ts("relu_c", lwb[:], 0.0, 1e-4, ALU.max, ALU.add)
+        regroup(0, "dve", 0, 2)
         wg = const.tile([P, 4 * HID], BF16, align_bytes=64)
         nc.vector.tensor_copy(
             out=wg[:].bitcast(F32).rearrange("p (c u) -> p c u", u=2), in_=wt[:].rearrange("p u c -> p c u")
         )
-        ab = stt("ab", th, -1.0, th, ALU.mult, ALU.max)
-        den = ts("den", ab, 4.0, 9.0, ALU.mult, ALU.add)
-        num = ts("num", ab, -4.0, 1.0, ALU.mult, ALU.add)
+        shift = small("shift")
+        nc.vector.tensor_scalar(out=shift[:], in0=cenb[:], scalar1=binb[:, 0:1], scalar2=None, op0=ALU.subtract)
         nc.vector.quantize_mx(out=wq[:].bitcast(FP8X4), scales=ws[:], in_=wg[:])
-        rden = small("rden")
-        nc.vector.reciprocal(out=rden[:], in_=den[:])
-        regroup(0, "dve", 0, 1)
-        s1 = tt("s1", num, rden)
-        regroup(0, "dve", 1, 2)
-        s2 = tt("s2", s1, s1)
-        regroup(0, "dve", 2, 3)
-        s4 = tt("s4", s2, s2)
-        p23 = ts("p23", s2, 1.0 / 7.0, 1.0 / 5.0, ALU.mult, ALU.add)
-        p01 = ts("p01", s2, 1.0 / 3.0, 1.0, ALU.mult, ALU.add)
-        regroup(0, "dve", 3, 4)
-        t1 = stt("t1", s4, 1.0 / 9.0, p23, ALU.mult, ALU.add)
-        s5 = tt("s5", s4, s1)
-        q01 = tt("q01", p01, s1)
+        regroup(0, "dve", 2, 4)
+        wid = tt("wid", lg[:], relu_c[:], ALU.add)
         quant_x(0)
         mm_z(0)
-        copy_z(0, "act")
-        hi = tt("hi", t1, s5)
-        lo = stt("lo", q01, 2.0, relu_c, ALU.mult, ALU.add)
-        wid = stt("wid", hi, 2.0, lo, ALU.mult, ALU.add)
+        inv = small("inv")
         nc.vector.reciprocal(out=inv[:], in_=wid[:])
-        nc.vector.scalar_tensor_tensor(out=nbias[:], in0=shift[:], scalar=-1.0, in1=inv[:], op0=ALU.mult, op1=ALU.mult)
-        nc.vector.tensor_tensor(out=inv2[:], in0=inv[:], in1=inv[:], op=ALU.mult)
+        w2r = tt("w2r", wid[:, R : R + 1], wid[:, R : R + 1], ALU.mult, 1)
+        inv2 = tt("inv2", inv[:], inv[:], ALU.mult)
 
-        scaled_gp(0)
+        def gp(nm, in0, in1):
+            t_new = small(nm)
+            nc.gpsimd.tensor_tensor(out=t_new[:], in0=in0[:], in1=in1[:], op=ALU.mult)
+            return t_new
+
+        dsh = small("dsh")
+        nc.gpsimd.tensor_scalar(
+            out=dsh[:], in0=shift[:], scalar1=-1.0, scalar2=shift[:, R : R + 1], op0=ALU.mult, op1=ALU.add
+        )
+        ua = small("ua")
+        nc.gpsimd.tensor_scalar(out=ua[:], in0=inv[:], scalar1=w2r[:, 0:1], scalar2=0.0, op0=ALU.mult, op1=ALU.add)
+        ub = gp("ub", dsh, inv)
+        va = gp("va", ua, inv)
+        vb = gp("vb", ub, inv)
+
+        copy_y(0)
+        factors_gp(0)
+        squares_act(0, 0)
+        regroup(1, "dve")
         quant_x(1)
         mm_z(1)
-        squares_act(0, 0)
         regroup(2, "dve")
-        copy_z(1, "dve")
-        scaled_gp(1)
+        copy_y(1)
+        factors_gp(1)
         squares_dve(0)
 
         ogs = []
@@ -296,23 +308,27 @@ def tile_rbfkanhead_t_kernel(tc, x, w_in, b_in, centers, log_widths, out_weight,
             oq.append(oq_g)
             osc.append(os_g)
 
+        copy_ow(0)
+        copy_ow(1)
+
         for it in range(NT):
             squares_act(it, 1)
             if it + 2 < NT:
                 quant_x(it + 2)
                 mm_z(it + 2)
             if it + 3 < NT:
-                regroup(it + 3, "dve")
+                regroup(it + 3, "dve", 0, TILES[it + 3][2] // 128 - gp_blocks(it + 3))
             if it >= 1:
                 quant_phi(it - 1, 1)
                 mm_out(it - 1, 1)
-            else:
-                copy_ow(0)
-                copy_ow(1)
             exp_act(it, 0)
             if it + 2 < NT:
-                copy_z(it + 2, "dve")
-                scaled_gp(it + 2)
+                copy_y(it + 2)
+                factors_gp(it + 2)
+            if it + 4 < NT:
+                n = TILES[it + 4][2] // 128
+                for q in range(n - gp_blocks(it + 4), n):
+                    regroup(it + 4, "gp", q, q + 1)
             if it + 1 < NT:
                 squares_dve(it + 1)
                 squares_act(it + 1, 0)

@@ -1,3 +1,4 @@
+import math
 from contextlib import ExitStack
 
 import concourse.masks as masks
@@ -23,16 +24,14 @@ R = 2
 
 def dve_planes(j):
     if j == 0:
-        return (6, 7)
+        return (R, 6)
     if j >= NT - 2:
         return (R, 3, 5, 6, 7)
-    return (R, 3, 5, 6, 7) if j % 4 == 0 else (R, 3, 6, 7)
+    return (R, 3, 6, 7)
 
 
 def gp_blocks(j):
-    if j < 5 or TILES[j][2] < PX:
-        return 0
-    return 1
+    return 0
 
 
 def tile_rbfkanhead_t_kernel(tc, x, w_in, b_in, centers, log_widths, out_weight, out_bias, out):
@@ -49,26 +48,28 @@ def tile_rbfkanhead_t_kernel(tc, x, w_in, b_in, centers, log_widths, out_weight,
         binb = const.tile([P, 1], BF16)
         obb = [const.tile([P, 1], BF16, name="ob%d" % h) for h in range(2)]
         w_sb = const.tile([P, C_IN], BF16)
-        xr = []
+        xr = {}
         for b in range(B):
-            xr.append(xin.tile([P, 4, HW], BF16, name="xr%d" % b))
+            for w0 in (0, PX) if b < 2 else (0,):
+                n = PX if b < 2 else HW
+                xr[(b, w0)] = xin.tile([P, 4, n], BF16, name="xr%d_%d" % (b, w0))
         xv = [x[b].rearrange("(p j) h w -> p j (h w)", j=4) for b in range(B)]
 
-        def load_x(b, lo, hi):
-            nc.sync.dma_start(out=xr[b][:, :, lo:hi], in_=xv[b][:, :, lo:hi])
+        def load_x(b, w0):
+            n = xr[(b, w0)].shape[2]
+            nc.sync.dma_start(out=xr[(b, w0)][:], in_=xv[b][:, :, w0 : w0 + n])
 
         with nc.allow_non_contiguous_dma(reason="small per-channel tables"):
             nc.sync.dma_start(out=lwb[:], in_=log_widths.rearrange("a c k x y -> (a c) (k x y)"))
-            load_x(0, 0, PX // 2)
+            load_x(0, 0)
             nc.sync.dma_start(out=w_sb[:], in_=w_in)
-            load_x(0, PX // 2, PX)
             nc.sync.dma_start(out=cenb[:], in_=centers.rearrange("a c k x y -> (a c) (k x y)"))
             nc.sync.dma_start(out=binb[:], in_=b_in.rearrange("(c o) -> c o", o=1))
             for h in range(2):
                 nc.scalar.dma_start(out=obb[h][:], in_=out_bias[h * P : (h + 1) * P].rearrange("(c o) -> c o", o=1))
-        load_x(0, PX, HW)
-        load_x(1, 0, PX)
-        load_x(1, PX, HW)
+        load_x(0, PX)
+        load_x(1, 0)
+        load_x(1, PX)
         ow_sb = []
         owv = out_weight.rearrange("o c k -> o (c k)")
         for h in range(2):
@@ -76,7 +77,7 @@ def tile_rbfkanhead_t_kernel(tc, x, w_in, b_in, centers, log_widths, out_weight,
             nc.sync.dma_start(out=t_ow[:], in_=owv[h * P : (h + 1) * P, :])
             ow_sb.append(t_ow)
         for b in range(2, B):
-            load_x(b, 0, HW)
+            load_x(b, 0)
         ident = const.tile([P, P], F32)
         masks.make_identity(nc, ident[:])
 
@@ -104,7 +105,8 @@ def tile_rbfkanhead_t_kernel(tc, x, w_in, b_in, centers, log_widths, out_weight,
             if j not in xgs:
                 xgs[j] = work.tile([P, 4 * n], BF16, tag="xg", name="xg", bufs=4, align_bytes=64)
             dst = xgs[j][:, 512 * q0 : 512 * q1]
-            src = xr[b][:, :, w0 + 128 * q0 : w0 + 128 * q1]
+            base = w0 if b < 2 else 0
+            src = xr[(b, base)][:, :, w0 - base + 128 * q0 : w0 - base + 128 * q1]
             if engine == "gp":
                 nc.gpsimd.tensor_scalar(
                     out=dst.rearrange("p (c t) -> p c t", t=4), in0=src.rearrange("p t c -> p c t"),
@@ -225,6 +227,11 @@ def tile_rbfkanhead_t_kernel(tc, x, w_in, b_in, centers, log_widths, out_weight,
             nc.vector.tensor_scalar(out=t_new[:], in0=in0, scalar1=c1, scalar2=c2, op0=op0, op1=op1)
             return t_new
 
+        def stt(nm, in0, c, in1, op0, op1):
+            t_new = small(nm)
+            nc.vector.scalar_tensor_tensor(out=t_new[:], in0=in0[:], scalar=c, in1=in1[:], op0=op0, op1=op1)
+            return t_new
+
         def tt(nm, in0, in1, op, cols=K):
             t_new = small(nm, cols)
             nc.vector.tensor_tensor(out=t_new[:], in0=in0, in1=in1, op=op)
@@ -232,29 +239,38 @@ def tile_rbfkanhead_t_kernel(tc, x, w_in, b_in, centers, log_widths, out_weight,
 
         mag = small("mag")
         nc.scalar.activation(out=mag[:], in_=lwb[:], func=ACT.Abs)
-        ex = small("ex")
-        nc.scalar.activation(out=ex[:], in_=mag[:], func=ACT.Exp, scale=-1.0)
-        lg = small("lg")
-        nc.scalar.activation(out=lg[:], in_=ex[:], func=ACT.Ln, bias=1.0, scale=1.0)
-        warm = small("warm")
-        nc.scalar.activation(out=warm[:], in_=mag[:], func=ACT.Exp, scale=-1.0)
-        relu_c = ts("relu_c", lwb[:], 0.0, 1e-4, ALU.max, ALU.add)
-        regroup(0, "dve", 0, 2)
+        a = small("a")
+        nc.scalar.activation(out=a[:], in_=mag[:], func=ACT.Tanh, scale=0.5)
+        relu_c = ts("relu_c", lwb[:], 0.0, math.log(1.6) + 1e-4, ALU.max, ALU.add)
+        den = ts("den", a[:], 4.0, 9.0, ALU.mult, ALU.add)
+        num = ts("num", a[:], -4.0, 1.0, ALU.mult, ALU.add)
+        rden = small("rden")
+        nc.vector.reciprocal(out=rden[:], in_=den[:])
+        s1 = tt("s1", num[:], rden[:], ALU.mult)
+        s2 = tt("s2", s1[:], s1[:], ALU.mult)
+        regroup(0, "dve", 0, 1)
+        h = stt("h1", s2, 9.0 / 7.0, s2, ALU.add, ALU.mult)
+        regroup(0, "dve", 1, 2)
+        h = stt("h2", h, 9.0 / 5.0, s2, ALU.add, ALU.mult)
+        regroup(0, "dve", 2, 3)
+        h = stt("h3", h, 9.0 / 3.0, s2, ALU.add, ALU.mult)
+        regroup(0, "dve", 3, 4)
+        h = stt("h4", h, 9.0, s1, ALU.add, ALU.mult)
         wg = const.tile([P, 4 * HID], BF16, align_bytes=64)
         nc.vector.tensor_copy(
             out=wg[:].bitcast(F32).rearrange("p (c u) -> p c u", u=2), in_=wt[:].rearrange("p u c -> p c u")
         )
+        wid = stt("wid", h, 2.0 / 9.0, relu_c, ALU.mult, ALU.add)
         shift = small("shift")
         nc.vector.tensor_scalar(out=shift[:], in0=cenb[:], scalar1=binb[:, 0:1], scalar2=None, op0=ALU.subtract)
         nc.vector.quantize_mx(out=wq[:].bitcast(FP8X4), scales=ws[:], in_=wg[:])
-        regroup(0, "dve", 2, 4)
-        wid = tt("wid", lg[:], relu_c[:], ALU.add)
-        quant_x(0)
-        mm_z(0)
         inv = small("inv")
         nc.vector.reciprocal(out=inv[:], in_=wid[:])
         w2r = tt("w2r", wid[:, R : R + 1], wid[:, R : R + 1], ALU.mult, 1)
+        quant_x(0)
+        mm_z(0)
         inv2 = tt("inv2", inv[:], inv[:], ALU.mult)
+        regroup(1, "act")
 
         def gp(nm, in0, in1):
             t_new = small(nm)
@@ -274,7 +290,6 @@ def tile_rbfkanhead_t_kernel(tc, x, w_in, b_in, centers, log_widths, out_weight,
         copy_y(0)
         factors_gp(0)
         squares_act(0, 0)
-        regroup(1, "dve")
         quant_x(1)
         mm_z(1)
         regroup(2, "dve")

@@ -19,6 +19,10 @@ FLOPS = 2 * B * HW * (C_IN * HID + HID * K * C_OUT)
 
 TILES = [(b, w0, PX) for b in range(B) for w0 in (0, PX)][:-1] + [(B - 1, PX, PX // 2), (B - 1, PX + PX // 2, PX // 2)]
 NT = len(TILES)
+CHUNKS = [(b, w0, PX) for b in range(2) for w0 in (0, PX)] + [(b, 0, HW) for b in range(2, B)]
+CHUNK_OF = [
+    [(c, w0 - cw, n) for c, (cb, cw, cn) in enumerate(CHUNKS) if cb == b and cw <= w0 < cw + cn][0] for b, w0, n in TILES
+]
 R = 2
 
 
@@ -27,11 +31,7 @@ def dve_planes(j):
         return (R, 6)
     if j >= NT - 2:
         return (R, 3, 5, 6, 7)
-    return (R, 3, 6, 7)
-
-
-def gp_blocks(j):
-    return 0
+    return (R, 3, 6) if j % 4 == 2 else (R, 3, 6, 7)
 
 
 def tile_rbfkanhead_t_kernel(tc, x, w_in, b_in, centers, log_widths, out_weight, out_bias, out):
@@ -48,36 +48,33 @@ def tile_rbfkanhead_t_kernel(tc, x, w_in, b_in, centers, log_widths, out_weight,
         binb = const.tile([P, 1], BF16)
         obb = [const.tile([P, 1], BF16, name="ob%d" % h) for h in range(2)]
         w_sb = const.tile([P, C_IN], BF16)
-        xr = {}
-        for b in range(B):
-            for w0 in (0, PX) if b < 2 else (0,):
-                n = PX if b < 2 else HW
-                xr[(b, w0)] = xin.tile([P, 4, n], BF16, name="xr%d_%d" % (b, w0))
+        xr = []
+        for c, (b, w0, n) in enumerate(CHUNKS):
+            xr.append(xin.tile([P, 4, n], BF16, name="xr%d" % c))
         xv = [x[b].rearrange("(p j) h w -> p j (h w)", j=4) for b in range(B)]
 
-        def load_x(b, w0):
-            n = xr[(b, w0)].shape[2]
-            nc.sync.dma_start(out=xr[(b, w0)][:], in_=xv[b][:, :, w0 : w0 + n])
+        def load_x(c):
+            b, w0, n = CHUNKS[c]
+            nc.sync.dma_start(out=xr[c][:], in_=xv[b][:, :, w0 : w0 + n])
 
         with nc.allow_non_contiguous_dma(reason="small per-channel tables"):
             nc.sync.dma_start(out=lwb[:], in_=log_widths.rearrange("a c k x y -> (a c) (k x y)"))
-            load_x(0, 0)
+            load_x(0)
             nc.sync.dma_start(out=w_sb[:], in_=w_in)
             nc.sync.dma_start(out=cenb[:], in_=centers.rearrange("a c k x y -> (a c) (k x y)"))
             nc.sync.dma_start(out=binb[:], in_=b_in.rearrange("(c o) -> c o", o=1))
             for h in range(2):
                 nc.scalar.dma_start(out=obb[h][:], in_=out_bias[h * P : (h + 1) * P].rearrange("(c o) -> c o", o=1))
-        load_x(0, PX)
-        load_x(1, 0)
-        load_x(1, PX)
+        for c in range(1, 4):
+            load_x(c)
         ow_sb = []
         owv = out_weight.rearrange("o c k -> o (c k)")
         for h in range(2):
             t_ow = const.tile([P, HID * K], BF16, name="ow_sb%d" % h)
             nc.sync.dma_start(out=t_ow[:], in_=owv[h * P : (h + 1) * P, :])
             ow_sb.append(t_ow)
-        for b in range(2, B):
-            load_x(b, 0)
+        for c in range(4, len(CHUNKS)):
+            load_x(c)
         ident = const.tile([P, P], F32)
         masks.make_identity(nc, ident[:])
 
@@ -95,44 +92,35 @@ def tile_rbfkanhead_t_kernel(tc, x, w_in, b_in, centers, log_widths, out_weight,
         vvs = {}
         sqs = {}
         phis = {}
-        pqs = {}
         ops = {}
 
-        def regroup(j, engine, q0=0, q1=None):
-            b, w0, n = TILES[j]
+        def regroup(c, engine="dve", q0=0, q1=None):
+            n = CHUNKS[c][2]
             if q1 is None:
                 q1 = n // 128
-            if j not in xgs:
-                xgs[j] = work.tile([P, 4 * n], BF16, tag="xg", name="xg", bufs=4, align_bytes=64)
-            dst = xgs[j][:, 512 * q0 : 512 * q1]
-            base = w0 if b < 2 else 0
-            src = xr[(b, base)][:, :, w0 - base + 128 * q0 : w0 - base + 128 * q1]
-            if engine == "gp":
-                nc.gpsimd.tensor_scalar(
-                    out=dst.rearrange("p (c t) -> p c t", t=4), in0=src.rearrange("p t c -> p c t"),
-                    scalar1=1.0, scalar2=0.0, op0=ALU.mult, op1=ALU.add,
-                )
-                return
-            dst = dst.rearrange("p (c i t) -> p c t i", i=4, t=4)
-            src = src.rearrange("p t (c i) -> p c t i", i=4)
+            if c not in xgs:
+                xgs[c] = work.tile([P, 4 * n], BF16, tag="xg", name="xg", align_bytes=64)
+            dst = xgs[c][:, 512 * q0 : 512 * q1].rearrange("p (c i t) -> p c t i", i=4, t=4)
+            src = xr[c][:, :, 128 * q0 : 128 * q1].rearrange("p t (c i) -> p c t i", i=4)
             if engine == "act":
                 nc.scalar.copy(out=dst, in_=src)
             else:
                 nc.vector.tensor_copy(out=dst, in_=src)
 
-        def quant_x(j):
-            n = TILES[j][2]
+        def quant_x(c):
+            n = CHUNKS[c][2]
             xq = work.tile([P, n], U32, tag="xq", align_bytes=64)
             xs = work.tile([P, n], U8, tag="xs", align_bytes=64)
-            nc.vector.quantize_mx(out=xq[:].bitcast(FP8X4), scales=xs[:], in_=xgs[j][:])
-            xqs[j] = (xq, xs)
+            nc.vector.quantize_mx(out=xq[:].bitcast(FP8X4), scales=xs[:], in_=xgs[c][:])
+            xqs[c] = (xq, xs)
 
         def mm_z(j):
-            xq, xs = xqs[j]
-            z_ps = psum.tile([P, TILES[j][2]], F32, tag="z", bufs=3)
+            c, o, n = CHUNK_OF[j]
+            xq, xs = xqs[c]
+            z_ps = psum.tile([P, n], F32, tag="z", bufs=3)
             nc.tensor.matmul_mx(
                 out=z_ps[:], lhsT=wq[:].bitcast(FP8X4), lhsT_scale=ws[:],
-                rhs=xq[:].bitcast(FP8X4), rhs_scale=xs[:], start=True, stop=True,
+                rhs=xq[:, o : o + n].bitcast(FP8X4), rhs_scale=xs[:, o : o + n], start=True, stop=True,
             )
             zs[j] = z_ps
 
@@ -179,32 +167,32 @@ def tile_rbfkanhead_t_kernel(tc, x, w_in, b_in, centers, log_widths, out_weight,
                     )
 
         def exp_act(j, g):
-            phi = work.tile([P, 4 * TILES[j][2]], BF16, tag="phi", align_bytes=64)
+            n = TILES[j][2]
+            if g == 0:
+                phis[j] = work.tile([P, 8 * n], BF16, tag="phi", name="phi", align_bytes=64)
             nc.scalar.activation(
-                out=phi[:].rearrange("p (c i t) -> p c t i", i=2, t=4),
+                out=phis[j][:, 4 * n * g : 4 * n * (g + 1)].rearrange("p (c i t) -> p c t i", i=2, t=4),
                 in_=sqs[(j, g)][:].rearrange("p (t c i) -> p c t i", t=4, i=2),
                 func=ACT.Exp, scale=-1.0,
             )
-            phis[(j, g)] = phi
 
-        def quant_phi(j, g):
+        def quant_phi(j, g0, g1):
             n = TILES[j][2]
-            pq = work.tile([P, n], U32, tag="pq", align_bytes=64)
-            ps = work.tile([P, n], U8, tag="ps", align_bytes=64)
-            nc.vector.quantize_mx(out=pq[:].bitcast(FP8X4), scales=ps[:], in_=phis[(j, g)][:])
-            pqs[(j, g)] = (pq, ps)
-
-        def mm_out(j, g):
-            pq, ps = pqs[(j, g)]
-            for h in range(2):
-                if g == 0:
-                    ops[(j, h)] = psum.tile([P, TILES[j][2]], F32, tag="o", bufs=4, name="o_ps")
-                nc.tensor.matmul_mx(
-                    out=ops[(j, h)][:],
-                    lhsT=oq[g][:, h * P : (h + 1) * P].bitcast(FP8X4),
-                    lhsT_scale=osc[g][:, h * P : (h + 1) * P],
-                    rhs=pq[:].bitcast(FP8X4), rhs_scale=ps[:], start=(g == 0), stop=(g == 1),
-                )
+            m = (g1 - g0) * n
+            pq = work.tile([P, m], U32, tag="pq", align_bytes=64)
+            ps = work.tile([P, m], U8, tag="ps", align_bytes=64)
+            nc.vector.quantize_mx(out=pq[:].bitcast(FP8X4), scales=ps[:], in_=phis[j][:, 4 * n * g0 : 4 * n * g1])
+            for g in range(g0, g1):
+                cols = slice(n * (g - g0), n * (g - g0 + 1))
+                for h in range(2):
+                    if g == 0:
+                        ops[(j, h)] = psum.tile([P, n], F32, tag="o", bufs=4, name="o_ps")
+                    nc.tensor.matmul_mx(
+                        out=ops[(j, h)][:],
+                        lhsT=oq[g][:, h * P : (h + 1) * P].bitcast(FP8X4),
+                        lhsT_scale=osc[g][:, h * P : (h + 1) * P],
+                        rhs=pq[:, cols].bitcast(FP8X4), rhs_scale=ps[:, cols], start=(g == 0), stop=(g == 1),
+                    )
 
         def evacuate(j, h, engine):
             b, w0, n = TILES[j]
@@ -252,9 +240,8 @@ def tile_rbfkanhead_t_kernel(tc, x, w_in, b_in, centers, log_widths, out_weight,
         h = stt("h1", s2, 9.0 / 7.0, s2, ALU.add, ALU.mult)
         regroup(0, "dve", 1, 2)
         h = stt("h2", h, 9.0 / 5.0, s2, ALU.add, ALU.mult)
-        regroup(0, "dve", 2, 3)
+        regroup(0, "act", 2, 4)
         h = stt("h3", h, 9.0 / 3.0, s2, ALU.add, ALU.mult)
-        regroup(0, "dve", 3, 4)
         h = stt("h4", h, 9.0, s1, ALU.add, ALU.mult)
         wg = const.tile([P, 4 * HID], BF16, align_bytes=64)
         nc.vector.tensor_copy(
@@ -292,7 +279,7 @@ def tile_rbfkanhead_t_kernel(tc, x, w_in, b_in, centers, log_widths, out_weight,
         squares_act(0, 0)
         quant_x(1)
         mm_z(1)
-        regroup(2, "dve")
+        regroup(2)
         copy_y(1)
         factors_gp(1)
         squares_dve(0)
@@ -329,27 +316,22 @@ def tile_rbfkanhead_t_kernel(tc, x, w_in, b_in, centers, log_widths, out_weight,
         for it in range(NT):
             squares_act(it, 1)
             if it + 2 < NT:
-                quant_x(it + 2)
+                if CHUNK_OF[it + 2][1] == 0:
+                    quant_x(CHUNK_OF[it + 2][0])
                 mm_z(it + 2)
-            if it + 3 < NT:
-                regroup(it + 3, "dve", 0, TILES[it + 3][2] // 128 - gp_blocks(it + 3))
+            if it + 3 < NT and CHUNK_OF[it + 3][1] == 0:
+                regroup(CHUNK_OF[it + 3][0])
             if it >= 1:
-                quant_phi(it - 1, 1)
-                mm_out(it - 1, 1)
+                quant_phi(it - 1, 0 if it + 1 < NT else 1, 2)
             exp_act(it, 0)
             if it + 2 < NT:
                 copy_y(it + 2)
                 factors_gp(it + 2)
-            if it + 4 < NT:
-                n = TILES[it + 4][2] // 128
-                for q in range(n - gp_blocks(it + 4), n):
-                    regroup(it + 4, "gp", q, q + 1)
             if it + 1 < NT:
                 squares_dve(it + 1)
                 squares_act(it + 1, 0)
             if it + 2 >= NT:
-                quant_phi(it, 0)
-                mm_out(it, 0)
+                quant_phi(it, 0, 1)
             if it >= 1:
                 evacuate(it - 1, 0, "dve")
                 evacuate(it - 1, 1, "dve")
@@ -357,10 +339,6 @@ def tile_rbfkanhead_t_kernel(tc, x, w_in, b_in, centers, log_widths, out_weight,
                 quant_ow(0)
                 quant_ow(1)
             exp_act(it, 1)
-            if it + 2 < NT:
-                quant_phi(it, 0)
-                mm_out(it, 0)
-        quant_phi(NT - 1, 1)
-        mm_out(NT - 1, 1)
+        quant_phi(NT - 1, 1, 2)
         evacuate(NT - 1, 0, "act")
         evacuate(NT - 1, 1, "dve")

@@ -17,9 +17,9 @@ P = 128
 PX = 512
 FLOPS = 2 * B * HW * (C_IN * HID + HID * K * C_OUT)
 
-TILES = [(b, w0, PX) for b in range(B) for w0 in (0, PX)][:-1] + [(B - 1, PX, PX // 2), (B - 1, PX + PX // 2, PX // 2)]
+TILES = [(0, 0, 256), (0, 256, 256)] + [(b, w0, PX) for b in range(B) for w0 in (0, PX)][1:-1] + [(B - 1, PX, 256), (B - 1, PX + 256, 256)]
 NT = len(TILES)
-CHUNKS = [(b, w0, PX) for b in range(2) for w0 in (0, PX)] + [(b, 0, HW) for b in range(2, B)]
+CHUNKS = TILES[:5] + [(b, 0, HW) for b in range(2, B)]
 CHUNK_OF = [
     [(c, w0 - cw, n) for c, (cb, cw, cn) in enumerate(CHUNKS) if cb == b and cw <= w0 < cw + cn][0] for b, w0, n in TILES
 ]
@@ -28,10 +28,14 @@ R = 2
 
 def dve_planes(j):
     if j == 0:
+        return (R,)
+    if j == 1:
         return (R, 6)
+    if j == 2:
+        return (R, 3, 6)
     if j >= NT - 2:
         return (R, 3, 5, 6, 7)
-    return (R, 3, 6) if j % 4 == 2 else (R, 3, 6, 7)
+    return (R, 3, 6, 7)
 
 
 def tile_rbfkanhead_t_kernel(tc, x, w_in, b_in, centers, log_widths, out_weight, out_bias, out):
@@ -61,11 +65,12 @@ def tile_rbfkanhead_t_kernel(tc, x, w_in, b_in, centers, log_widths, out_weight,
             nc.sync.dma_start(out=lwb[:], in_=log_widths.rearrange("a c k x y -> (a c) (k x y)"))
             load_x(0)
             nc.sync.dma_start(out=w_sb[:], in_=w_in)
+            load_x(1)
             nc.sync.dma_start(out=cenb[:], in_=centers.rearrange("a c k x y -> (a c) (k x y)"))
             nc.sync.dma_start(out=binb[:], in_=b_in.rearrange("(c o) -> c o", o=1))
             for h in range(2):
                 nc.scalar.dma_start(out=obb[h][:], in_=out_bias[h * P : (h + 1) * P].rearrange("(c o) -> c o", o=1))
-        for c in range(1, 4):
+        for c in range(2, 5):
             load_x(c)
         ow_sb = []
         owv = out_weight.rearrange("o c k -> o (c k)")
@@ -73,7 +78,7 @@ def tile_rbfkanhead_t_kernel(tc, x, w_in, b_in, centers, log_widths, out_weight,
             t_ow = const.tile([P, HID * K], BF16, name="ow_sb%d" % h)
             nc.sync.dma_start(out=t_ow[:], in_=owv[h * P : (h + 1) * P, :])
             ow_sb.append(t_ow)
-        for c in range(4, len(CHUNKS)):
+        for c in range(5, len(CHUNKS)):
             load_x(c)
         ident = const.tile([P, P], F32)
         masks.make_identity(nc, ident[:])
@@ -229,35 +234,38 @@ def tile_rbfkanhead_t_kernel(tc, x, w_in, b_in, centers, log_widths, out_weight,
         nc.scalar.activation(out=mag[:], in_=lwb[:], func=ACT.Abs)
         a = small("a")
         nc.scalar.activation(out=a[:], in_=mag[:], func=ACT.Tanh, scale=0.5)
-        relu_c = ts("relu_c", lwb[:], 0.0, math.log(1.6) + 1e-4, ALU.max, ALU.add)
+        relu_c = small("relu_c")
+        nc.gpsimd.tensor_scalar(
+            out=relu_c[:], in0=lwb[:], scalar1=0.0, scalar2=math.log(1.6) + 1e-4, op0=ALU.max, op1=ALU.add
+        )
         den = ts("den", a[:], 4.0, 9.0, ALU.mult, ALU.add)
         num = ts("num", a[:], -4.0, 1.0, ALU.mult, ALU.add)
         rden = small("rden")
         nc.vector.reciprocal(out=rden[:], in_=den[:])
+        regroup(0, "act", 1, 2)
         s1 = tt("s1", num[:], rden[:], ALU.mult)
-        s2 = tt("s2", s1[:], s1[:], ALU.mult)
         regroup(0, "dve", 0, 1)
-        h = stt("h1", s2, 9.0 / 7.0, s2, ALU.add, ALU.mult)
-        regroup(0, "dve", 1, 2)
-        h = stt("h2", h, 9.0 / 5.0, s2, ALU.add, ALU.mult)
-        regroup(0, "act", 2, 4)
-        h = stt("h3", h, 9.0 / 3.0, s2, ALU.add, ALU.mult)
-        h = stt("h4", h, 9.0, s1, ALU.add, ALU.mult)
+        s2 = tt("s2", s1[:], s1[:], ALU.mult)
         wg = const.tile([P, 4 * HID], BF16, align_bytes=64)
         nc.vector.tensor_copy(
             out=wg[:].bitcast(F32).rearrange("p (c u) -> p c u", u=2), in_=wt[:].rearrange("p u c -> p c u")
         )
-        wid = stt("wid", h, 2.0 / 9.0, relu_c, ALU.mult, ALU.add)
+        h = stt("h1", s2, 9.0 / 7.0, s2, ALU.add, ALU.mult)
+        nc.vector.quantize_mx(out=wq[:].bitcast(FP8X4), scales=ws[:], in_=wg[:])
+        h = stt("h2", h, 9.0 / 5.0, s2, ALU.add, ALU.mult)
+        quant_x(0)
+        mm_z(0)
+        regroup(1, "act")
+        regroup(2, "act", 2, 4)
+        h = stt("h3", h, 9.0 / 3.0, s2, ALU.add, ALU.mult)
         shift = small("shift")
         nc.vector.tensor_scalar(out=shift[:], in0=cenb[:], scalar1=binb[:, 0:1], scalar2=None, op0=ALU.subtract)
-        nc.vector.quantize_mx(out=wq[:].bitcast(FP8X4), scales=ws[:], in_=wg[:])
+        h = stt("h4", h, 9.0, s1, ALU.add, ALU.mult)
+        wid = stt("wid", h, 2.0 / 9.0, relu_c, ALU.mult, ALU.add)
         inv = small("inv")
         nc.vector.reciprocal(out=inv[:], in_=wid[:])
         w2r = tt("w2r", wid[:, R : R + 1], wid[:, R : R + 1], ALU.mult, 1)
-        quant_x(0)
-        mm_z(0)
         inv2 = tt("inv2", inv[:], inv[:], ALU.mult)
-        regroup(1, "act")
 
         def gp(nm, in0, in1):
             t_new = small(nm)
@@ -279,7 +287,7 @@ def tile_rbfkanhead_t_kernel(tc, x, w_in, b_in, centers, log_widths, out_weight,
         squares_act(0, 0)
         quant_x(1)
         mm_z(1)
-        regroup(2)
+        regroup(2, "dve", 0, 2)
         copy_y(1)
         factors_gp(1)
         squares_dve(0)
@@ -310,9 +318,6 @@ def tile_rbfkanhead_t_kernel(tc, x, w_in, b_in, centers, log_widths, out_weight,
             oq.append(oq_g)
             osc.append(os_g)
 
-        copy_ow(0)
-        copy_ow(1)
-
         for it in range(NT):
             squares_act(it, 1)
             if it + 2 < NT:
@@ -321,6 +326,9 @@ def tile_rbfkanhead_t_kernel(tc, x, w_in, b_in, centers, log_widths, out_weight,
                 mm_z(it + 2)
             if it + 3 < NT and CHUNK_OF[it + 3][1] == 0:
                 regroup(CHUNK_OF[it + 3][0])
+            if it == 1:
+                quant_ow(0)
+                quant_ow(1)
             if it >= 1:
                 quant_phi(it - 1, 0 if it + 1 < NT else 1, 2)
             exp_act(it, 0)
@@ -336,8 +344,8 @@ def tile_rbfkanhead_t_kernel(tc, x, w_in, b_in, centers, log_widths, out_weight,
                 evacuate(it - 1, 0, "dve")
                 evacuate(it - 1, 1, "dve")
             else:
-                quant_ow(0)
-                quant_ow(1)
+                copy_ow(0)
+                copy_ow(1)
             exp_act(it, 1)
         quant_phi(NT - 1, 1, 2)
         evacuate(NT - 1, 0, "act")

@@ -33,7 +33,7 @@ def dve_planes(j):
         return (R, 6)
     if j == 2:
         return (R, 3, 6)
-    if j >= NT - 2:
+    if j >= NT - 3:
         return (R, 3, 5, 6, 7)
     return (R, 3, 6, 7)
 
@@ -78,7 +78,7 @@ def tile_rbfkanhead_t_kernel(tc, x, w_in, b_in, centers, log_widths, out_weight,
             t_ow = const.tile([P, HID * K], BF16, name="ow_sb%d" % h)
             nc.sync.dma_start(out=t_ow[:], in_=owv[h * P : (h + 1) * P, :])
             ow_sb.append(t_ow)
-        for c in range(5, len(CHUNKS)):
+        for c in range(5, 7):
             load_x(c)
         ident = const.tile([P, P], F32)
         masks.make_identity(nc, ident[:])
@@ -230,10 +230,9 @@ def tile_rbfkanhead_t_kernel(tc, x, w_in, b_in, centers, log_widths, out_weight,
             nc.vector.tensor_tensor(out=t_new[:], in0=in0, in1=in1, op=op)
             return t_new
 
-        mag = small("mag")
-        nc.scalar.activation(out=mag[:], in_=lwb[:], func=ACT.Abs)
-        a = small("a")
-        nc.scalar.activation(out=a[:], in_=mag[:], func=ACT.Tanh, scale=0.5)
+        th = small("th")
+        nc.scalar.activation(out=th[:], in_=lwb[:], func=ACT.Tanh, scale=0.5)
+        a = stt("a", th, -1.0, th, ALU.mult, ALU.max)
         relu_c = small("relu_c")
         nc.gpsimd.tensor_scalar(
             out=relu_c[:], in0=lwb[:], scalar1=0.0, scalar2=math.log(1.6) + 1e-4, op0=ALU.max, op1=ALU.add
@@ -261,6 +260,8 @@ def tile_rbfkanhead_t_kernel(tc, x, w_in, b_in, centers, log_widths, out_weight,
         shift = small("shift")
         nc.vector.tensor_scalar(out=shift[:], in0=cenb[:], scalar1=binb[:, 0:1], scalar2=None, op0=ALU.subtract)
         h = stt("h4", h, 9.0, s1, ALU.add, ALU.mult)
+        quant_x(1)
+        mm_z(1)
         wid = stt("wid", h, 2.0 / 9.0, relu_c, ALU.mult, ALU.add)
         inv = small("inv")
         nc.vector.reciprocal(out=inv[:], in_=wid[:])
@@ -285,9 +286,9 @@ def tile_rbfkanhead_t_kernel(tc, x, w_in, b_in, centers, log_widths, out_weight,
         copy_y(0)
         factors_gp(0)
         squares_act(0, 0)
-        quant_x(1)
-        mm_z(1)
         regroup(2, "dve", 0, 2)
+        quant_x(2)
+        mm_z(2)
         copy_y(1)
         factors_gp(1)
         squares_dve(0)
@@ -320,7 +321,7 @@ def tile_rbfkanhead_t_kernel(tc, x, w_in, b_in, centers, log_widths, out_weight,
 
         for it in range(NT):
             squares_act(it, 1)
-            if it + 2 < NT:
+            if 0 < it < NT - 2:
                 if CHUNK_OF[it + 2][1] == 0:
                     quant_x(CHUNK_OF[it + 2][0])
                 mm_z(it + 2)
@@ -346,6 +347,8 @@ def tile_rbfkanhead_t_kernel(tc, x, w_in, b_in, centers, log_widths, out_weight,
             else:
                 copy_ow(0)
                 copy_ow(1)
+            if it + 5 < NT and CHUNK_OF[it + 5][1] == 0 and CHUNK_OF[it + 5][0] >= 7:
+                load_x(CHUNK_OF[it + 5][0])
             exp_act(it, 1)
         quant_phi(NT - 1, 1, 2)
         evacuate(NT - 1, 0, "act")

@@ -28,12 +28,12 @@ R = 2
 
 def dve_planes(j):
     if j == 0:
-        return (R,)
+        return ()
     if j == 1:
         return (R, 6)
     if j == 2:
         return (R, 3, 6)
-    if j >= NT - 3:
+    if j >= NT - 4:
         return (R, 3, 5, 6, 7)
     return (R, 3, 6, 7)
 
@@ -52,13 +52,15 @@ def tile_rbfkanhead_t_kernel(tc, x, w_in, b_in, centers, log_widths, out_weight,
         binb = const.tile([P, 1], BF16)
         obb = [const.tile([P, 1], BF16, name="ob%d" % h) for h in range(2)]
         w_sb = const.tile([P, C_IN], BF16)
-        xr = []
-        for c, (b, w0, n) in enumerate(CHUNKS):
-            xr.append(xin.tile([P, 4, n], BF16, name="xr%d" % c))
+        xr = {}
         xv = [x[b].rearrange("(p j) h w -> p j (h w)", j=4) for b in range(B)]
 
         def load_x(c):
             b, w0, n = CHUNKS[c]
+            if c < 2:
+                xr[c] = xin.tile([P, 4, n], BF16, name="xr%d" % c)
+            else:
+                xr[c] = xin.tile([P, 4, n], BF16, tag="xr", name="xr", bufs=3)
             nc.sync.dma_start(out=xr[c][:], in_=xv[b][:, :, w0 : w0 + n])
 
         with nc.allow_non_contiguous_dma(reason="small per-channel tables"):
@@ -78,8 +80,6 @@ def tile_rbfkanhead_t_kernel(tc, x, w_in, b_in, centers, log_widths, out_weight,
             t_ow = const.tile([P, HID * K], BF16, name="ow_sb%d" % h)
             nc.sync.dma_start(out=t_ow[:], in_=owv[h * P : (h + 1) * P, :])
             ow_sb.append(t_ow)
-        for c in range(5, 7):
-            load_x(c)
         ident = const.tile([P, P], F32)
         masks.make_identity(nc, ident[:])
 
@@ -165,11 +165,12 @@ def tile_rbfkanhead_t_kernel(tc, x, w_in, b_in, centers, log_widths, out_weight,
 
         def squares_act(j, g):
             for k in range(4 * g, 4 * g + 4):
-                if k not in dve_planes(j):
-                    nc.scalar.activation(
-                        out=plane(j, k), in_=ys[j][:], func=ACT.Square,
-                        bias=ub[:, k : k + 1], scale=ua[:, k : k + 1],
-                    )
+                if k in dve_planes(j):
+                    continue
+                src, bias, scale = (ys[j], ub, ua) if j > 0 else (zs[j], nbias, inv)
+                nc.scalar.activation(
+                    out=plane(j, k), in_=src[:], func=ACT.Square, bias=bias[:, k : k + 1], scale=scale[:, k : k + 1]
+                )
 
         def exp_act(j, g):
             n = TILES[j][2]
@@ -265,6 +266,7 @@ def tile_rbfkanhead_t_kernel(tc, x, w_in, b_in, centers, log_widths, out_weight,
         wid = stt("wid", h, 2.0 / 9.0, relu_c, ALU.mult, ALU.add)
         inv = small("inv")
         nc.vector.reciprocal(out=inv[:], in_=wid[:])
+        nbias = stt("nbias", shift, -1.0, inv, ALU.mult, ALU.mult)
         w2r = tt("w2r", wid[:, R : R + 1], wid[:, R : R + 1], ALU.mult, 1)
         inv2 = tt("inv2", inv[:], inv[:], ALU.mult)
 
@@ -283,15 +285,13 @@ def tile_rbfkanhead_t_kernel(tc, x, w_in, b_in, centers, log_widths, out_weight,
         va = gp("va", ua, inv)
         vb = gp("vb", ub, inv)
 
-        copy_y(0)
-        factors_gp(0)
         squares_act(0, 0)
         regroup(2, "dve", 0, 2)
+        load_x(5)
         quant_x(2)
         mm_z(2)
         copy_y(1)
         factors_gp(1)
-        squares_dve(0)
 
         ogs = []
         ot_pss = []
@@ -327,6 +327,8 @@ def tile_rbfkanhead_t_kernel(tc, x, w_in, b_in, centers, log_widths, out_weight,
                 mm_z(it + 2)
             if it + 3 < NT and CHUNK_OF[it + 3][1] == 0:
                 regroup(CHUNK_OF[it + 3][0])
+                if CHUNK_OF[it + 3][0] + 3 < len(CHUNKS):
+                    load_x(CHUNK_OF[it + 3][0] + 3)
             if it == 1:
                 quant_ow(0)
                 quant_ow(1)
@@ -347,8 +349,6 @@ def tile_rbfkanhead_t_kernel(tc, x, w_in, b_in, centers, log_widths, out_weight,
             else:
                 copy_ow(0)
                 copy_ow(1)
-            if it + 5 < NT and CHUNK_OF[it + 5][1] == 0 and CHUNK_OF[it + 5][0] >= 7:
-                load_x(CHUNK_OF[it + 5][0])
             exp_act(it, 1)
         quant_phi(NT - 1, 1, 2)
         evacuate(NT - 1, 0, "act")

@@ -167,7 +167,7 @@ def tile_rbfkanhead_t_kernel(tc, x, w_in, b_in, centers, log_widths, out_weight,
             for k in range(4 * g, 4 * g + 4):
                 if k in dve_planes(j):
                     continue
-                src, bias, scale = (ys[j], ub, ua) if j > 0 else (zs[j], nbias, inv)
+                src, bias, scale = (ys[j], nub, nua) if j > 0 else (zs[j], nbias, inv)
                 nc.scalar.activation(
                     out=plane(j, k), in_=src[:], func=ACT.Square, bias=bias[:, k : k + 1], scale=scale[:, k : k + 1]
                 )
@@ -270,24 +270,13 @@ def tile_rbfkanhead_t_kernel(tc, x, w_in, b_in, centers, log_widths, out_weight,
         w2r = tt("w2r", wid[:, R : R + 1], wid[:, R : R + 1], ALU.mult, 1)
         inv2 = tt("inv2", inv[:], inv[:], ALU.mult)
 
-        def gp(nm, in0, in1):
-            t_new = small(nm)
-            nc.gpsimd.tensor_tensor(out=t_new[:], in0=in0[:], in1=in1[:], op=ALU.mult)
-            return t_new
-
-        dsh = small("dsh")
-        nc.gpsimd.tensor_scalar(
-            out=dsh[:], in0=shift[:], scalar1=-1.0, scalar2=shift[:, R : R + 1], op0=ALU.mult, op1=ALU.add
-        )
-        ua = small("ua")
-        nc.gpsimd.tensor_scalar(out=ua[:], in0=inv[:], scalar1=w2r[:, 0:1], scalar2=0.0, op0=ALU.mult, op1=ALU.add)
-        ub = gp("ub", dsh, inv)
-        va = gp("va", ua, inv)
-        vb = gp("vb", ub, inv)
-
         squares_act(0, 0)
         regroup(2, "dve", 0, 2)
         load_x(5)
+        nub = stt("nub", shift, shift[:, R : R + 1], inv, ALU.subtract, ALU.mult)
+        nua = ts("nua", inv[:], w2r[:, 0:1], -1.0, ALU.mult, ALU.mult)
+        vb = stt("vb", nub, -1.0, inv, ALU.mult, ALU.mult)
+        va = stt("va", nua, -1.0, inv, ALU.mult, ALU.mult)
         quant_x(2)
         mm_z(2)
         copy_y(1)

@@ -33,7 +33,7 @@ def dve_planes(j):
         return (R, 6)
     if j == 2:
         return (R, 3, 6)
-    if j >= NT - 4:
+    if j >= NT - 3:
         return (R, 3, 5, 6, 7)
     return (R, 3, 6, 7)
 
@@ -139,10 +139,10 @@ def tile_rbfkanhead_t_kernel(tc, x, w_in, b_in, centers, log_widths, out_weight,
 
         def plane(j, k):
             n = TILES[j][2]
-            g = k // 4
-            if (j, g) not in sqs:
-                sqs[(j, g)] = work.tile([P, 4 * n], F32, tag="sq", bufs=5, name="sq")
-            return sqs[(j, g)][:, (k % 4) * n : (k % 4 + 1) * n]
+            if j not in sqs:
+                sqs[j] = work.tile([P, K * n], F32, tag="sq", name="sq")
+            o = (2 * (k % 4) + k // 4) * n
+            return sqs[j][:, o : o + n]
 
         def factors_gp(j):
             for k in dve_planes(j):
@@ -172,14 +172,19 @@ def tile_rbfkanhead_t_kernel(tc, x, w_in, b_in, centers, log_widths, out_weight,
                     out=plane(j, k), in_=src[:], func=ACT.Square, bias=bias[:, k : k + 1], scale=scale[:, k : k + 1]
                 )
 
-        def exp_act(j, g):
+        def exp_act(j, groups):
             n = TILES[j][2]
-            if g == 0:
+            if j not in phis:
                 phis[j] = work.tile([P, 8 * n], BF16, tag="phi", name="phi", align_bytes=64)
+            dst = phis[j][:]
+            src = sqs[j][:]
+            if len(groups) == 1:
+                dst = dst[:, 4 * n * groups[0] : 4 * n * (groups[0] + 1)]
+                src = src.rearrange("p (t g c i) -> p g c t i", t=4, g=2, i=2)[:, groups[0]]
+            else:
+                src = src.rearrange("p (t c i) -> p c t i", t=4, i=2)
             nc.scalar.activation(
-                out=phis[j][:, 4 * n * g : 4 * n * (g + 1)].rearrange("p (c i t) -> p c t i", i=2, t=4),
-                in_=sqs[(j, g)][:].rearrange("p (t c i) -> p c t i", t=4, i=2),
-                func=ACT.Exp, scale=-1.0,
+                out=dst.rearrange("p (c i t) -> p c t i", i=2, t=4), in_=src, func=ACT.Exp, scale=-1.0
             )
 
         def quant_phi(j, g0, g1):
@@ -271,6 +276,7 @@ def tile_rbfkanhead_t_kernel(tc, x, w_in, b_in, centers, log_widths, out_weight,
         inv2 = tt("inv2", inv[:], inv[:], ALU.mult)
 
         squares_act(0, 0)
+        squares_act(0, 1)
         regroup(2, "dve", 0, 2)
         load_x(5)
         nub = stt("nub", shift, shift[:, R : R + 1], inv, ALU.subtract, ALU.mult)
@@ -309,7 +315,6 @@ def tile_rbfkanhead_t_kernel(tc, x, w_in, b_in, centers, log_widths, out_weight,
             osc.append(os_g)
 
         for it in range(NT):
-            squares_act(it, 1)
             if 0 < it < NT - 2:
                 if CHUNK_OF[it + 2][1] == 0:
                     quant_x(CHUNK_OF[it + 2][0])
@@ -323,13 +328,15 @@ def tile_rbfkanhead_t_kernel(tc, x, w_in, b_in, centers, log_widths, out_weight,
                 quant_ow(1)
             if it >= 1:
                 quant_phi(it - 1, 0 if it + 1 < NT else 1, 2)
-            exp_act(it, 0)
+            if it >= NT - 2:
+                exp_act(it, (0,))
             if it + 2 < NT:
                 copy_y(it + 2)
                 factors_gp(it + 2)
             if it + 1 < NT:
                 squares_dve(it + 1)
                 squares_act(it + 1, 0)
+                squares_act(it + 1, 1)
             if it + 2 >= NT:
                 quant_phi(it, 0, 1)
             if it >= 1:
@@ -338,7 +345,7 @@ def tile_rbfkanhead_t_kernel(tc, x, w_in, b_in, centers, log_widths, out_weight,
             else:
                 copy_ow(0)
                 copy_ow(1)
-            exp_act(it, 1)
+            exp_act(it, (0, 1) if it < NT - 2 else (1,))
         quant_phi(NT - 1, 1, 2)
         evacuate(NT - 1, 0, "act")
         evacuate(NT - 1, 1, "dve")

import math
from contextlib import ExitStack

import concourse.masks as masks
import concourse.mybir as mybir

F32 = mybir.dt.float32
BF16 = mybir.dt.bfloat16
U32 = mybir.dt.uint32
U8 = mybir.dt.uint8
FP8X4 = mybir.dt.float8_e4m3fn_x4
ACT = mybir.ActivationFunctionType
ALU = mybir.AluOpType

B, C_IN, HW, HID, K, C_OUT = 8, 512, 1024, 128, 8, 256
P = 128
PX = 512
FLOPS = 2 * B * HW * (C_IN * HID + HID * K * C_OUT)

TILES = [(0, 0, 256), (0, 256, 256)] + [(b, w0, PX) for b in range(B) for w0 in (0, PX)][1:-1] + [(B - 1, PX, 256), (B - 1, PX + 256, 256)]
NT = len(TILES)
CHUNKS = TILES[:5] + [(b, 0, HW) for b in range(2, B)]
CHUNK_OF = [
    [(c, w0 - cw, n) for c, (cb, cw, cn) in enumerate(CHUNKS) if cb == b and cw <= w0 < cw + cn][0] for b, w0, n in TILES
]
R = 2


def dve_planes(j):
    if j == 0:
        return ()
    if j == 1:
        return (R, 6)
    if j == 2:
        return (R, 3, 6)
    if j >= NT - 3:
        return (R, 3, 5, 6, 7)
    return (R, 3, 6, 7)


def tile_rbfkanhead_t_kernel(tc, x, w_in, b_in, centers, log_widths, out_weight, out_bias, out):
    nc = tc.nc
    with ExitStack() as ctx:
        const = ctx.enter_context(tc.tile_pool(name="const", bufs=1))
        xin = ctx.enter_context(tc.tile_pool(name="xin", bufs=1))
        work = ctx.enter_context(tc.tile_pool(name="work", bufs=3))
        psum = ctx.enter_context(tc.psum_pool(name="psum", bufs=2))
        ctx.enter_context(tc.manual_schedule())

        lwb = const.tile([P, K], BF16)
        cenb = const.tile([P, K], BF16)
        binb = const.tile([P, 1], BF16)
        obb = [const.tile([P, 1], BF16, name="ob%d" % h) for h in range(2)]
        w_sb = const.tile([P, C_IN], BF16)
        xr = {}
        xv = [x[b].rearrange("(p j) h w -> p j (h w)", j=4) for b in range(B)]

        def load_x(c):
            b, w0, n = CHUNKS[c]
            if c < 2:
                xr[c] = xin.tile([P, 4, n], BF16, name="xr%d" % c)
            else:
                xr[c] = xin.tile([P, 4, n], BF16, tag="xr", name="xr", bufs=3)
            nc.sync.dma_start(out=xr[c][:], in_=xv[b][:, :, w0 : w0 + n])

        with nc.allow_non_contiguous_dma(reason="small per-channel tables"):
            nc.sync.dma_start(out=lwb[:], in_=log_widths.rearrange("a c k x y -> (a c) (k x y)"))
            load_x(0)
            nc.sync.dma_start(out=w_sb[:], in_=w_in)
            load_x(1)
            nc.sync.dma_start(out=cenb[:], in_=centers.rearrange("a c k x y -> (a c) (k x y)"))
            nc.sync.dma_start(out=binb[:], in_=b_in.rearrange("(c o) -> c o", o=1))
            for h in range(2):
                nc.scalar.dma_start(out=obb[h][:], in_=out_bias[h * P : (h + 1) * P].rearrange("(c o) -> c o", o=1))
        for c in range(2, 5):
            load_x(c)
        ow_sb = []
        owv = out_weight.rearrange("o c k -> o (c k)")
        for h in range(2):
            t_ow = const.tile([P, HID * K], BF16, name="ow_sb%d" % h)
            nc.sync.dma_start(out=t_ow[:], in_=owv[h * P : (h + 1) * P, :])
            ow_sb.append(t_ow)
        ident = const.tile([P, P], F32)
        masks.make_identity(nc, ident[:])

        def small(nm, cols=K):
            return const.tile([P, cols], F32, name=nm)

        wq = const.tile([P, HID], U32, align_bytes=64)
        ws = const.tile([P, HID], U8, align_bytes=64)
        oq = []
        osc = []
        xgs = {}
        xqs = {}
        zs = {}
        ys = {}
        vvs = {}
        sqs = {}
        phis = {}
        ops = {}

        def regroup(c, engine="dve", q0=0, q1=None):
            n = CHUNKS[c][2]
            if q1 is None:
                q1 = n // 128
            if c not in xgs:
                xgs[c] = work.tile([P, 4 * n], BF16, tag="xg", name="xg", align_bytes=64)
            dst = xgs[c][:, 512 * q0 : 512 * q1].rearrange("p (c i t) -> p c t i", i=4, t=4)
            src = xr[c][:, :, 128 * q0 : 128 * q1].rearrange("p t (c i) -> p c t i", i=4)
            if engine == "act":
                nc.scalar.copy(out=dst, in_=src)
            else:
                nc.vector.tensor_copy(out=dst, in_=src)

        def quant_x(c):
            n = CHUNKS[c][2]
            xq = work.tile([P, n], U32, tag="xq", align_bytes=64)
            xs = work.tile([P, n], U8, tag="xs", align_bytes=64)
            nc.vector.quantize_mx(out=xq[:].bitcast(FP8X4), scales=xs[:], in_=xgs[c][:])
            xqs[c] = (xq, xs)

        def mm_z(j):
            c, o, n = CHUNK_OF[j]
            xq, xs = xqs[c]
            z_ps = psum.tile([P, n], F32, tag="z", bufs=3)
            nc.tensor.matmul_mx(
                out=z_ps[:], lhsT=wq[:].bitcast(FP8X4), lhsT_scale=ws[:],
                rhs=xq[:, o : o + n].bitcast(FP8X4), rhs_scale=xs[:, o : o + n], start=True, stop=True,
            )
            zs[j] = z_ps

        def copy_y(j):
            y = work.tile([P, TILES[j][2]], F32, tag="y", bufs=4)
            nc.vector.tensor_scalar(
                out=y[:], in0=zs[j][:], scalar1=shift[:, R : R + 1], scalar2=inv2[:, R : R + 1],
                op0=ALU.subtract, op1=ALU.mult,
            )
            ys[j] = y

        def plane(j, k):
            n = TILES[j][2]
            if j not in sqs:
                sqs[j] = work.tile([P, K * n], F32, tag="sq", name="sq")
            o = (2 * (k % 4) + k // 4) * n
            return sqs[j][:, o : o + n]

        def factors_gp(j):
            for k in dve_planes(j):
                if k == R:
                    continue
                vv = work.tile([P, TILES[j][2]], F32, tag="vv", bufs=9)
                nc.gpsimd.tensor_scalar(
                    out=vv[:], in0=ys[j][:], scalar1=va[:, k : k + 1], scalar2=vb[:, k : k + 1],
                    op0=ALU.mult, op1=ALU.add,
                )
                vvs[(j, k)] = vv

        def squares_dve(j):
            for k in dve_planes(j):
                factor = ys[j] if k == R else vvs[(j, k)]
                nc.vector.scalar_tensor_tensor(
                    out=plane(j, k), in0=zs[j][:], scalar=shift[:, k : k + 1],
                    in1=factor[:], op0=ALU.subtract, op1=ALU.mult,
                )

        def squares_act(j, g):
            for k in range(4 * g, 4 * g + 4):
                if k in dve_planes(j):
                    continue
                src, bias, scale = (ys[j], nub, nua) if j > 0 else (zs[j], nbias, inv)
                nc.scalar.activation(
                    out=plane(j, k), in_=src[:], func=ACT.Square, bias=bias[:, k : k + 1], scale=scale[:, k : k + 1]
                )

        def exp_act(j, groups):
            n = TILES[j][2]
            if j not in phis:
                phis[j] = work.tile([P, 8 * n], BF16, tag="phi", name="phi", align_bytes=64)
            dst = phis[j][:]
            src = sqs[j][:]
            if len(groups) == 1:
                dst = dst[:, 4 * n * groups[0] : 4 * n * (groups[0] + 1)]
                src = src.rearrange("p (t g c i) -> p g c t i", t=4, g=2, i=2)[:, groups[0]]
            else:
                src = src.rearrange("p (t c i) -> p c t i", t=4, i=2)
            nc.scalar.activation(
                out=dst.rearrange("p (c i t) -> p c t i", i=2, t=4), in_=src, func=ACT.Exp, scale=-1.0
            )

        def quant_phi(j, g0, g1):
            n = TILES[j][2]
            m = (g1 - g0) * n
            pq = work.tile([P, m], U32, tag="pq", align_bytes=64)
            ps = work.tile([P, m], U8, tag="ps", align_bytes=64)
            nc.vector.quantize_mx(out=pq[:].bitcast(FP8X4), scales=ps[:], in_=phis[j][:, 4 * n * g0 : 4 * n * g1])
            for g in range(g0, g1):
                cols = slice(n * (g - g0), n * (g - g0 + 1))
                for h in range(2):
                    if g == 0:
                        ops[(j, h)] = psum.tile([P, n], F32, tag="o", bufs=4, name="o_ps")
                    nc.tensor.matmul_mx(
                        out=ops[(j, h)][:],
                        lhsT=oq[g][:, h * P : (h + 1) * P].bitcast(FP8X4),
                        lhsT_scale=osc[g][:, h * P : (h + 1) * P],
                        rhs=pq[:, cols].bitcast(FP8X4), rhs_scale=ps[:, cols], start=(g == 0), stop=(g == 1),
                    )

        def evacuate(j, h, engine):
            b, w0, n = TILES[j]
            o_sb = work.tile([P, n], F32, tag="o_sb", bufs=6)
            if engine == "act":
                nc.scalar.activation(out=o_sb[:], in_=ops[(j, h)][:], func=ACT.Identity, bias=obb[h][:, 0:1], scale=1.0)
            else:
                nc.vector.tensor_scalar(out=o_sb[:], in0=ops[(j, h)][:], scalar1=obb[h][:, 0:1], scalar2=None, op0=ALU.add)
            nc.sync.dma_start(
                out=out[b, h * P : (h + 1) * P].rearrange("o h w -> o (h w)")[:, w0 : w0 + n], in_=o_sb[:]
            )

        wt = psum.tile([P, 2, P], F32, tag="o", bufs=4)
        w_words = w_sb[:].bitcast(F32).rearrange("c (p u) -> c u p", u=2)
        for u in range(2):
            nc.tensor.transpose(out=wt[:, u, :], in_=w_words[:, u, :], identity=ident[:])

        def ts(nm, in0, c1, c2, op0, op1):
            t_new = small(nm)
            nc.vector.tensor_scalar(out=t_new[:], in0=in0, scalar1=c1, scalar2=c2, op0=op0, op1=op1)
            return t_new

        def stt(nm, in0, c, in1, op0, op1):
            t_new = small(nm)
            nc.vector.scalar_tensor_tensor(out=t_new[:], in0=in0[:], scalar=c, in1=in1[:], op0=op0, op1=op1)
            return t_new

        def tt(nm, in0, in1, op, cols=K):
            t_new = small(nm, cols)
            nc.vector.tensor_tensor(out=t_new[:], in0=in0, in1=in1, op=op)
            return t_new

        th = small("th")
        nc.scalar.activation(out=th[:], in_=lwb[:], func=ACT.Tanh, scale=0.5)
        a = stt("a", th, -1.0, th, ALU.mult, ALU.max)
        relu_c = small("relu_c")
        nc.gpsimd.tensor_scalar(
            out=relu_c[:], in0=lwb[:], scalar1=0.0, scalar2=math.log(1.6) + 1e-4, op0=ALU.max, op1=ALU.add
        )
        den = ts("den", a[:], 4.0, 9.0, ALU.mult, ALU.add)
        num = ts("num", a[:], -4.0, 1.0, ALU.mult, ALU.add)
        rden = small("rden")
        nc.vector.reciprocal(out=rden[:], in_=den[:])
        regroup(0, "act", 1, 2)
        s1 = tt("s1", num[:], rden[:], ALU.mult)
        regroup(0, "dve", 0, 1)
        s2 = tt("s2", s1[:], s1[:], ALU.mult)
        wg = const.tile([P, 4 * HID], BF16, align_bytes=64)
        nc.vector.tensor_copy(
            out=wg[:].bitcast(F32).rearrange("p (c u) -> p c u", u=2), in_=wt[:].rearrange("p u c -> p c u")
        )
        h = stt("h1", s2, 9.0 / 7.0, s2, ALU.add, ALU.mult)
        nc.vector.quantize_mx(out=wq[:].bitcast(FP8X4), scales=ws[:], in_=wg[:])
        h = stt("h2", h, 9.0 / 5.0, s2, ALU.add, ALU.mult)
        quant_x(0)
        mm_z(0)
        regroup(1, "act")
        regroup(2, "act", 2, 4)
        h = stt("h3", h, 9.0 / 3.0, s2, ALU.add, ALU.mult)
        shift = small("shift")
        nc.vector.tensor_scalar(out=shift[:], in0=cenb[:], scalar1=binb[:, 0:1], scalar2=None, op0=ALU.subtract)
        h = stt("h4", h, 9.0, s1, ALU.add, ALU.mult)
        quant_x(1)
        mm_z(1)
        wid = stt("wid", h, 2.0 / 9.0, relu_c, ALU.mult, ALU.add)
        inv = small("inv")
        nc.vector.reciprocal(out=inv[:], in_=wid[:])
        nbias = stt("nbias", shift, -1.0, inv, ALU.mult, ALU.mult)
        w2r = tt("w2r", wid[:, R : R + 1], wid[:, R : R + 1], ALU.mult, 1)
        inv2 = tt("inv2", inv[:], inv[:], ALU.mult)

        squares_act(0, 0)
        squares_act(0, 1)
        regroup(2, "dve", 0, 2)
        load_x(5)
        nub = stt("nub", shift, shift[:, R : R + 1], inv, ALU.subtract, ALU.mult)
        nua = ts("nua", inv[:], w2r[:, 0:1], -1.0, ALU.mult, ALU.mult)
        vb = stt("vb", nub, -1.0, inv, ALU.mult, ALU.mult)
        va = stt("va", nua, -1.0, inv, ALU.mult, ALU.mult)
        quant_x(2)
        mm_z(2)
        copy_y(1)
        factors_gp(1)

        ogs = []
        ot_pss = []
        for g in range(2):
            ot_ps = psum.tile([P, 2, C_OUT], F32, tag="o", bufs=4)
            for u in range(2):
                for h in range(2):
                    words = ow_sb[h][:].bitcast(F32).rearrange("o (c q) -> o q c", q=4)
                    nc.tensor.transpose(
                        out=ot_ps[:, u, h * P : (h + 1) * P], in_=words[:, 2 * g + u, :], identity=ident[:]
                    )
            ot_pss.append(ot_ps)

        def copy_ow(g):
            og = const.tile([P, 4 * C_OUT], BF16, name="og%d" % g, align_bytes=64)
            nc.vector.tensor_copy(
                out=og[:].bitcast(F32).rearrange("p (m u) -> p m u", u=2), in_=ot_pss[g][:].rearrange("p u m -> p m u")
            )
            ogs.append(og)

        def quant_ow(g):
            oq_g = const.tile([P, C_OUT], U32, name="oq%d" % g, align_bytes=64)
            os_g = const.tile([P, C_OUT], U8, name="os%d" % g, align_bytes=64)
            nc.vector.quantize_mx(out=oq_g[:].bitcast(FP8X4), scales=os_g[:], in_=ogs[g][:])
            oq.append(oq_g)
            osc.append(os_g)

        for it in range(NT):
            if 0 < it < NT - 2:
                if CHUNK_OF[it + 2][1] == 0:
                    quant_x(CHUNK_OF[it + 2][0])
                mm_z(it + 2)
            if it + 3 < NT and CHUNK_OF[it + 3][1] == 0:
                regroup(CHUNK_OF[it + 3][0])
                if CHUNK_OF[it + 3][0] + 3 < len(CHUNKS):
                    load_x(CHUNK_OF[it + 3][0] + 3)
            if it == 1:
                quant_ow(0)
                quant_ow(1)
            if it >= 1:
                quant_phi(it - 1, 0 if it + 1 < NT else 1, 2)
            if it >= NT - 2:
                exp_act(it, (0,))
            if it + 2 < NT:
                copy_y(it + 2)
                factors_gp(it + 2)
            if it + 1 < NT:
                squares_dve(it + 1)
                squares_act(it + 1, 0)
                squares_act(it + 1, 1)
            if it + 2 >= NT:
                quant_phi(it, 0, 1)
            if it >= 1:
                evacuate(it - 1, 0, "dve")
                evacuate(it - 1, 1, "dve")
            else:
                copy_ow(0)
                copy_ow(1)
            exp_act(it, (0, 1) if it < NT - 2 else (1,))
        quant_phi(NT - 1, 1, 2)
        evacuate(NT - 1, 0, "act")
        evacuate(NT - 1, 1, "dve")
